import numpy as np
import ml_dtypes


def mxq(x, axis, fmt="e4m3"):
    dtype, down = {"e4m3": (ml_dtypes.float8_e4m3fn, 7), "e5m2": (ml_dtypes.float8_e5m2, 14)}[fmt]
    v = np.moveaxis(np.asarray(x, np.float32).astype(ml_dtypes.bfloat16).astype(np.float64), axis, -1)
    blocks = v.reshape(v.shape[:-1] + (-1, 32))
    amax = np.abs(blocks).max(-1, keepdims=True)
    byte = np.maximum(np.where(amax > 0, np.frexp(amax)[1] - 1 + 127, 0) - down, 1)
    scale = np.exp2(byte - 127.0)
    codes = (blocks / scale).astype(np.float32).astype(dtype).astype(np.float64)
    return np.moveaxis((codes * scale).reshape(v.shape), -1, axis)


WIDE = False


def mx_kscale(k):
    if not WIDE:
        return np.ones(k)
    levels = np.array([10, -10, 5, -5, 0])
    a = np.random.permutation(np.resize(levels, k // 512 * 4)).reshape(k // 512, 4)
    idx = np.arange(k)
    return np.exp2(a[idx // 512, idx % 128 // 32])


BF16 = ml_dtypes.bfloat16


def bf(x):
    return np.asarray(x, np.float32).astype(BF16)


def f64(x):
    return np.asarray(x).astype(np.float64)


BB, S, P, J, K, M, L, N, C = 2, 512, 2, 4, 4, 512, 64, 512, 4
B = BB * S
R = P * K * L


def setup_inputs():
    t = mx_kscale(R).reshape(P, K, L)[:, :, 0][:, None, :, None, None]
    gy = np.exp2(np.random.uniform(-1.0, 1.0, (P, J, K, 1, 1)))
    gz = np.exp2(np.random.uniform(-1.0, 1.0, (P, J, K, 1, 1)))
    return {"x_q": bf(np.random.standard_normal((BB, S, K * N))),
            "Y_fp": bf(np.random.standard_normal((P, J, K, M, L)) * gy / np.sqrt(R) / t),
            "Z_fp": bf(np.random.standard_normal((P, J, K, L, N)) * gz / np.sqrt(N) * t),
            "a_core": bf(np.random.standard_normal((P, J, K)))}


def reference(x_q, Y_fp, Z_fp, a_core):
    Y, Z = f64(Y_fp), f64(Z_fp)
    Y_scale = np.mean(np.abs(Y), axis=(-2, -1), keepdims=True)
    Z_scale = np.mean(np.abs(Z), axis=(-2, -1), keepdims=True)
    Y_q = np.abs(Y_scale) * np.sign(Y)
    Z_q = np.abs(Z_scale) * np.sign(Z)
    Xk = f64(x_q).reshape(B, K, N).transpose(1, 0, 2)
    Zk = Z_q.transpose(2, 4, 0, 1, 3).reshape(K, N, P * J * L)
    T = mxq(Xk, 2, 'e4m3') @ mxq(Zk, 1, 'e4m3')
    Tj = T.reshape(K, B, P, J, L).transpose(3, 1, 2, 0, 4).reshape(J, B, R)
    Wj = (f64(a_core)[..., None, None] * Y_q).transpose(1, 0, 2, 4, 3).reshape(J, R, M)
    out1 = mxq(Tj, 2, 'e4m3') @ mxq(Wj, 1, 'e4m3')
    return out1.transpose(1, 0, 2)

@@ -1,0 +1,301 @@
+from contextlib import ExitStack
+
+import concourse.mybir as mybir
+from concourse.masks import make_identity
+
+BF16 = mybir.dt.bfloat16
+F32 = mybir.dt.float32
+U32 = mybir.dt.uint32
+U8 = mybir.dt.uint8
+I32 = mybir.dt.int32
+FP8X4 = mybir.dt.float8_e4m3fn_x4
+ACT = mybir.ActivationFunctionType
+ALU = mybir.AluOpType
+AX = mybir.AxisListType
+
+P = 128
+NP, NJ, NK = 2, 4, 4
+M, L, N = 512, 64, 512
+B = 1024
+B_TILES = B // P
+BLOCK_ELEMS = M * L
+CLEAR_SIGNS = 0x7FFF7FFF
+FLOPS = 2 * (2 * B * N * NP * NJ * NK * L)
+
+
+def tile_bqqlinear_pa_kernel(tc, x_q, Y_fp, Z_fp, a_core, out):
+    nc = tc.nc
+    x_rows = x_q.flatten_outer_dims()
+    out_rows = out.rearrange("b j m -> b (j m)")
+    z_tiles = Z_fp.rearrange("p j k l n -> (p j k l) n").rearrange("(i r) n -> r i n", r=P)
+
+    with ExitStack() as ctx:
+        const = ctx.enter_context(tc.tile_pool(name="const", bufs=1))
+        work = ctx.enter_context(tc.tile_pool(name="work", bufs=2))
+        psum = ctx.enter_context(tc.psum_pool(name="psum", bufs=2))
+
+        ident_f = const.tile([P, P], F32)
+        make_identity(nc, ident_f[:])
+        perm_f = const.tile([P, P], F32)
+        nc.vector.tensor_copy(
+            out=perm_f[:].rearrange("i (h v lam d) -> i h v lam d", h=2, v=2, d=2),
+            in_=ident_f[:].rearrange("i (h lam v d) -> i h v lam d", h=2, v=2, d=2),
+        )
+        half_mask = const.tile([P, 2 * P], F32)
+        nc.vector.memset(half_mask[:], 0.0)
+        nc.vector.memset(half_mask[0:64, 0:P], 1.0)
+        nc.vector.memset(half_mask[64:P, P : 2 * P], 1.0)
+        ones_f = const.tile([P, P], F32)
+        nc.vector.memset(ones_f[:], 1.0)
+        pick_half = const.tile([P, 16 * 32], BF16)
+        nc.vector.memset(pick_half[:], 0.0)
+        nc.vector.memset(pick_half[0:64, 0 : 16 * 32 : 34], 1.0)
+        nc.vector.memset(pick_half[64:P, 1 : 16 * 32 : 34], 1.0)
+        pick_all = const.tile([P, 16 * 16], BF16)
+        nc.vector.memset(pick_all[:], 0.0)
+        nc.vector.memset(pick_all[:, 0 : 16 * 16 : 17], 1.0)
+        group_of = const.tile([P, 8], F32)
+        nc.vector.tensor_reduce(
+            out=group_of[:], in_=ident_f[:].rearrange("q (g lam) -> q g lam", g=8), axis=AX.X, op=ALU.add
+        )
+
+        z_sb = const.tile([P, 16 * N], BF16)
+        for g in range(4):
+            nc.sync.dma_start(
+                out=z_sb[:, g * 4 * N : (g + 1) * 4 * N].rearrange("r (i n) -> r i n", n=N),
+                in_=z_tiles[:, g * 4 : (g + 1) * 4, :],
+            )
+        x_sb = [const.tile([P, NK * N], BF16, name="x_sb%d" % bt) for bt in range(B_TILES)]
+
+        def load_x(bt):
+            nc.sync.dma_start(out=x_sb[bt][:], in_=x_rows[bt * P : (bt + 1) * P, :])
+
+        load_x(0)
+        load_x(1)
+        a_all = const.tile([P, NP * NJ * NK], BF16)
+        nc.sync.dma_start(out=a_all[:], in_=a_core.rearrange("p j k -> (p j k)").partition_broadcast(P))
+        y_sb = const.tile([P, NJ * 4 * 8 * L], BF16)
+        y_view = y_sb[:].rearrange("r (j mc g l) -> r j mc g l", j=NJ, mc=4, g=8)
+        with nc.allow_non_contiguous_dma(reason="rows of 64 bfloat16 values"):
+            for j in range(NJ):
+                for k in range(NK):
+                    for p in range(NP):
+                        nc.sync.dma_start(
+                            out=y_view[:, j, :, k * NP + p, :],
+                            in_=Y_fp[p, j, k].rearrange("(mc r) l -> r mc l", r=P),
+                        )
+        for bt in range(2, B_TILES):
+            load_x(bt)
+
+        z_acc = psum.tile([P, 512], F32, tag="t")
+        for g in range(4):
+            mag = work.tile([P, 4 * N], BF16, tag="mag")
+            nc.vector.tensor_scalar(
+                out=mag[:].bitcast(I32),
+                in0=z_sb[:, g * 4 * N : (g + 1) * 4 * N].bitcast(I32),
+                scalar1=CLEAR_SIGNS,
+                scalar2=None,
+                op0=ALU.bitwise_and,
+            )
+            for s in range(16):
+                i = g * 4 + s // 4
+                nc.tensor.matmul(
+                    out=z_acc[:, 0:32],
+                    lhsT=mag[:, s * P : (s + 1) * P],
+                    rhs=pick_half[:, i * 32 : (i + 1) * 32],
+                    start=(g == 0 and s == 0),
+                    stop=(g == 3 and s == 15),
+                )
+        z_cols = const.tile([P, 32], F32)
+        nc.vector.tensor_copy(out=z_cols[:], in_=z_acc[:, 0:32])
+        z_tot = psum.tile([P, 512], F32, tag="o")
+        nc.tensor.matmul(out=z_tot[:, 0:32], lhsT=ones_f[:], rhs=z_cols[:], start=True, stop=True)
+        zs = const.tile([P, 32], F32)
+        nc.vector.tensor_scalar(
+            out=zs[:], in0=z_tot[:, 0:32], scalar1=1.0 / BLOCK_ELEMS, scalar2=None, op0=ALU.mult
+        )
+        z_words = z_sb[:].bitcast(F32)
+        z_grouped = const.tile([P, NK * 2048], BF16, align_bytes=64)
+        for pj in range(NP * NJ):
+            p, j = pj // NJ, pj % NJ
+            zt = psum.tile([P, 512], F32, tag="xt")
+            for u in range(2):
+                for kh in range(2):
+                    first = (pj * 2 + kh) * 256 + u * P
+                    nc.tensor.transpose(
+                        zt[:, (u * 2 + kh) * P : (u * 2 + kh + 1) * P], z_words[:, first : first + P], perm_f[:]
+                    )
+            nc.scalar.activation(
+                out=z_grouped[:].rearrange("q (k j v p x u e) -> q k j v p x u e", k=NK, j=NJ, v=2, p=NP, x=32, u=2)[
+                    :, :, j, :, p, :, :, :
+                ],
+                in_=zt[:].bitcast(BF16).rearrange("q (u k v x e) -> q k v x u e", u=2, k=NK, v=2, x=32),
+                func=ACT.Sign,
+            )
+            for k in range(NK):
+                z_part = z_grouped[:].rearrange("q (k j v p y) -> q k j v p y", k=NK, j=NJ, v=2, p=NP)[:, k, j, :, p, :]
+                nc.vector.tensor_scalar(
+                    out=z_part,
+                    in0=z_part,
+                    scalar1=zs[:, pj * NK + k : pj * NK + k + 1],
+                    scalar2=None,
+                    op0=ALU.mult,
+                )
+        z_codes = const.tile([P, NK * 512], U32, align_bytes=64)
+        z_scales = const.tile([P, NK * 512], U8, align_bytes=64)
+        for k in range(NK):
+            nc.vector.quantize_mx(
+                out=z_codes[:, k * 512 : (k + 1) * 512].bitcast(FP8X4),
+                scales=z_scales[:, k * 512 : (k + 1) * 512],
+                in_=z_grouped[:, k * 2048 : (k + 1) * 2048],
+            )
+
+        def quantise_x(bt):
+            x_words = x_sb[bt][:].bitcast(F32)
+            x_grouped = work.tile([P, NK * P * 4], BF16, align_bytes=64)
+            x_grouped_words = x_grouped[:].bitcast(F32)
+            for kh in range(2):
+                xt = psum.tile([P, 512], F32, tag="xt")
+                for s in range(4):
+                    first = kh * 512 + s * P
+                    nc.tensor.transpose(xt[:, s * P : (s + 1) * P], x_words[:, first : first + P], ident_f[:])
+                nc.vector.tensor_copy(
+                    out=x_grouped_words[:, kh * 512 : (kh + 1) * 512].rearrange("q (kk b u) -> q kk b u", kk=2, u=2),
+                    in_=xt[:].rearrange("q (kk u b) -> q kk b u", kk=2, u=2),
+                )
+            x_codes = work.tile([P, NK * P], U32, align_bytes=64, bufs=3)
+            x_scales = work.tile([P, NK * P], U8, align_bytes=64, bufs=3)
+            nc.vector.quantize_mx(out=x_codes[:].bitcast(FP8X4), scales=x_scales[:], in_=x_grouped[:])
+            return x_codes, x_scales
+
+        x_ready = {0: quantise_x(0), 1: quantise_x(1)}
+
+        y_acc = psum.tile([P, 512], F32, tag="o")
+        for j in range(NJ):
+            mag = work.tile([P, 4 * N], BF16, tag="mag")
+            nc.vector.tensor_scalar(
+                out=mag[:].bitcast(I32),
+                in0=y_sb[:, j * 2048 : (j + 1) * 2048].bitcast(I32),
+                scalar1=CLEAR_SIGNS,
+                scalar2=None,
+                op0=ALU.bitwise_and,
+            )
+            for s in range(16):
+                nc.tensor.matmul(
+                    out=y_acc[:, 0:16],
+                    lhsT=mag[:, s * P : (s + 1) * P],
+                    rhs=pick_all[:, (j * NK + s % NK) * 16 : (j * NK + s % NK + 1) * 16],
+                    start=(j == 0 and s == 0),
+                    stop=(j == NJ - 1 and s == 15),
+                )
+        y_cols = const.tile([P, 16], F32)
+        nc.vector.tensor_copy(out=y_cols[:], in_=y_acc[:, 0:16])
+        y_tot = psum.tile([P, 512], F32, tag="o")
+        for p in range(NP):
+            nc.tensor.matmul(
+                out=y_tot[:, p * 16 : (p + 1) * 16],
+                lhsT=half_mask[:, p * P : (p + 1) * P],
+                rhs=y_cols[:],
+                start=True,
+                stop=True,
+            )
+        gain = const.tile([P, 32], F32)
+        nc.vector.scalar_tensor_tensor(
+            out=gain[:], in0=y_tot[:, 0:32], scalar=1.0 / BLOCK_ELEMS, in1=a_all[:], op0=ALU.mult, op1=ALU.mult
+        )
+        own_gain = const.tile([P, 32], F32)
+        nc.vector.tensor_tensor(
+            out=own_gain[:].rearrange("q (j k p) -> q j k p", j=NJ, k=NK),
+            in0=gain[:].rearrange("q (p j k) -> q j k p", p=NP, j=NJ),
+            in1=group_of[:].rearrange("q (k p) -> q k p", k=NK).unsqueeze(1).to_broadcast([P, NJ, NK, NP]),
+            op=ALU.mult,
+        )
+        w_gain = const.tile([P, NJ], F32)
+        nc.vector.tensor_reduce(
+            out=w_gain[:], in_=own_gain[:].rearrange("q (j g) -> q j g", j=NJ), axis=AX.X, op=ALU.add
+        )
+        y_words = y_sb[:].bitcast(F32)
+        w_grouped = const.tile([P, NJ * 2048], BF16, align_bytes=64)
+        w_codes = const.tile([P, NJ * 512], U32, align_bytes=64)
+        w_scales = const.tile([P, NJ * 512], U8, align_bytes=64)
+        for j in range(NJ):
+            for mh in range(2):
+                yt = psum.tile([P, 512], F32, tag="xt")
+                for u in range(2):
+                    for mcc in range(2):
+                        first = (j * 4 + mh * 2 + mcc) * 256
+                        nc.tensor.transpose(
+                            yt[:, (u * 2 + mcc) * P : (u * 2 + mcc + 1) * P],
+                            y_words[:, first + u : first + 256 : 2],
+                            ident_f[:],
+                        )
+                nc.scalar.activation(
+                    out=w_grouped[:, (j * 2 + mh) * 1024 : (j * 2 + mh + 1) * 1024].rearrange(
+                        "q (m u e) -> q m u e", u=2, e=2
+                    ),
+                    in_=yt[:].bitcast(BF16).rearrange("q (u m e) -> q m u e", u=2, e=2),
+                    func=ACT.Sign,
+                )
+            nc.vector.tensor_scalar(
+                out=w_grouped[:, j * 2048 : (j + 1) * 2048],
+                in0=w_grouped[:, j * 2048 : (j + 1) * 2048],
+                scalar1=w_gain[:, j : j + 1],
+                scalar2=None,
+                op0=ALU.mult,
+            )
+            nc.vector.quantize_mx(
+                out=w_codes[:, j * 512 : (j + 1) * 512].bitcast(FP8X4),
+                scales=w_scales[:, j * 512 : (j + 1) * 512],
+                in_=w_grouped[:, j * 2048 : (j + 1) * 2048],
+            )
+
+        for bt in range(B_TILES):
+            x_codes, x_scales = x_ready[bt]
+            t_rows = work.tile([P, 2048], BF16)
+            t_rows_view = t_rows[:].rearrange("b (jv k y) -> b jv k y", jv=8, k=NK)
+            t_words = t_rows[:].bitcast(F32)
+            for k in range(NK):
+                t_ps = psum.tile([P, 512], F32, tag="t")
+                nc.tensor.matmul_mx(
+                    out=t_ps[:],
+                    lhsT=x_codes[:, k * P : (k + 1) * P].bitcast(FP8X4),
+                    lhsT_scale=x_scales[:, k * P : (k + 1) * P],
+                    rhs=z_codes[:, k * 512 : (k + 1) * 512].bitcast(FP8X4),
+                    rhs_scale=z_scales[:, k * 512 : (k + 1) * 512],
+                    start=True,
+                    stop=True,
+                )
+                nc.scalar.copy(out=t_rows_view[:, :, k, :], in_=t_ps[:].rearrange("b (jv y) -> b jv y", jv=8))
+            if bt + 2 < B_TILES:
+                x_ready[bt + 2] = quantise_x(bt + 2)
+            t_grouped = work.tile([P, 2048], BF16, align_bytes=64)
+            t_grouped_words = t_grouped[:].bitcast(F32)
+            for jh in range(2):
+                tt = psum.tile([P, 512], F32, tag="tt")
+                for s in range(4):
+                    first = (jh * 4 + s) * P
+                    nc.tensor.transpose(tt[:, s * P : (s + 1) * P], t_words[:, first : first + P], ident_f[:])
+                nc.vector.tensor_copy(
+                    out=t_grouped_words[:, jh * 512 : (jh + 1) * 512].rearrange("q (jj b v) -> q jj b v", jj=2, v=2),
+                    in_=tt[:].rearrange("q (jj v b) -> q jj b v", jj=2, v=2),
+                )
+            t_codes = work.tile([P, NJ * P], U32, align_bytes=64)
+            t_scales = work.tile([P, NJ * P], U8, align_bytes=64)
+            nc.vector.quantize_mx(out=t_codes[:].bitcast(FP8X4), scales=t_scales[:], in_=t_grouped[:])
+            o_sb = work.tile([P, NJ * M], F32, bufs=3)
+            for j in range(NJ):
+                o_ps = psum.tile([P, 512], F32, tag="o")
+                nc.tensor.matmul_mx(
+                    out=o_ps[:],
+                    lhsT=t_codes[:, j * P : (j + 1) * P].bitcast(FP8X4),
+                    lhsT_scale=t_scales[:, j * P : (j + 1) * P],
+                    rhs=w_codes[:, j * 512 : (j + 1) * 512].bitcast(FP8X4),
+                    rhs_scale=w_scales[:, j * 512 : (j + 1) * 512],
+                    start=True,
+                    stop=True,
+                )
+                if j == 0:
+                    nc.vector.tensor_copy(out=o_sb[:, j * M : (j + 1) * M], in_=o_ps[:])
+                else:
+                    nc.scalar.copy(out=o_sb[:, j * M : (j + 1) * M], in_=o_ps[:])
+            nc.sync.dma_start(out=out_rows[bt * P : (bt + 1) * P, :], in_=o_sb[:])

@@ -20,6 +20,7 @@ B = 1024
 B_TILES = B // P
 BLOCK_ELEMS = M * L
 CLEAR_SIGNS = 0x7FFF7FFF
+PREP_ITEMS = 8
 FLOPS = 2 * (2 * B * N * NP * NJ * NK * L)
 
 
@@ -32,48 +33,17 @@ def tile_bqqlinear_pa_kernel(tc, x_q, Y_fp, Z_fp, a_core, out):
     with ExitStack() as ctx:
         const = ctx.enter_context(tc.tile_pool(name="const", bufs=1))
         work = ctx.enter_context(tc.tile_pool(name="work", bufs=2))
-        psum = ctx.enter_context(tc.psum_pool(name="psum", bufs=2))
+        psum = ctx.enter_context(tc.psum_pool(name="psum", bufs=4))
+        ctx.enter_context(tc.manual_schedule())
 
-        ident_f = const.tile([P, P], F32)
-        make_identity(nc, ident_f[:])
-        perm_f = const.tile([P, P], F32)
-        nc.vector.tensor_copy(
-            out=perm_f[:].rearrange("i (h v lam d) -> i h v lam d", h=2, v=2, d=2),
-            in_=ident_f[:].rearrange("i (h lam v d) -> i h v lam d", h=2, v=2, d=2),
-        )
-        half_mask = const.tile([P, 2 * P], F32)
-        nc.vector.memset(half_mask[:], 0.0)
-        nc.vector.memset(half_mask[0:64, 0:P], 1.0)
-        nc.vector.memset(half_mask[64:P, P : 2 * P], 1.0)
-        ones_f = const.tile([P, P], F32)
-        nc.vector.memset(ones_f[:], 1.0)
-        pick_half = const.tile([P, 16 * 32], BF16)
-        nc.vector.memset(pick_half[:], 0.0)
-        nc.vector.memset(pick_half[0:64, 0 : 16 * 32 : 34], 1.0)
-        nc.vector.memset(pick_half[64:P, 1 : 16 * 32 : 34], 1.0)
-        pick_all = const.tile([P, 16 * 16], BF16)
-        nc.vector.memset(pick_all[:], 0.0)
-        nc.vector.memset(pick_all[:, 0 : 16 * 16 : 17], 1.0)
-        group_of = const.tile([P, 8], F32)
-        nc.vector.tensor_reduce(
-            out=group_of[:], in_=ident_f[:].rearrange("q (g lam) -> q g lam", g=8), axis=AX.X, op=ALU.add
-        )
-
+        a_all = const.tile([P, NP * NJ * NK], BF16)
+        nc.scalar.dma_start(out=a_all[:], in_=a_core.rearrange("p j k -> (p j k)").partition_broadcast(P))
         z_sb = const.tile([P, 16 * N], BF16)
         for g in range(4):
             nc.sync.dma_start(
                 out=z_sb[:, g * 4 * N : (g + 1) * 4 * N].rearrange("r (i n) -> r i n", n=N),
                 in_=z_tiles[:, g * 4 : (g + 1) * 4, :],
             )
-        x_sb = [const.tile([P, NK * N], BF16, name="x_sb%d" % bt) for bt in range(B_TILES)]
-
-        def load_x(bt):
-            nc.sync.dma_start(out=x_sb[bt][:], in_=x_rows[bt * P : (bt + 1) * P, :])
-
-        load_x(0)
-        load_x(1)
-        a_all = const.tile([P, NP * NJ * NK], BF16)
-        nc.sync.dma_start(out=a_all[:], in_=a_core.rearrange("p j k -> (p j k)").partition_broadcast(P))
         y_sb = const.tile([P, NJ * 4 * 8 * L], BF16)
         y_view = y_sb[:].rearrange("r (j mc g l) -> r j mc g l", j=NJ, mc=4, g=8)
         with nc.allow_non_contiguous_dma(reason="rows of 64 bfloat16 values"):
@@ -84,218 +54,300 @@ def tile_bqqlinear_pa_kernel(tc, x_q, Y_fp, Z_fp, a_core, out):
                             out=y_view[:, j, :, k * NP + p, :],
                             in_=Y_fp[p, j, k].rearrange("(mc r) l -> r mc l", r=P),
                         )
-        for bt in range(2, B_TILES):
-            load_x(bt)
+        x_sb = [const.tile([P, NK * N], BF16, name="x_sb%d" % n) for n in range(B_TILES)]
+        for n in range(B_TILES):
+            nc.sync.dma_start(out=x_sb[n][:], in_=x_rows[n * P : (n + 1) * P, :])
 
-        z_acc = psum.tile([P, 512], F32, tag="t")
-        for g in range(4):
-            mag = work.tile([P, 4 * N], BF16, tag="mag")
-            nc.vector.tensor_scalar(
-                out=mag[:].bitcast(I32),
-                in0=z_sb[:, g * 4 * N : (g + 1) * 4 * N].bitcast(I32),
-                scalar1=CLEAR_SIGNS,
-                scalar2=None,
-                op0=ALU.bitwise_and,
-            )
-            for s in range(16):
-                i = g * 4 + s // 4
-                nc.tensor.matmul(
-                    out=z_acc[:, 0:32],
-                    lhsT=mag[:, s * P : (s + 1) * P],
-                    rhs=pick_half[:, i * 32 : (i + 1) * 32],
-                    start=(g == 0 and s == 0),
-                    stop=(g == 3 and s == 15),
-                )
-        z_cols = const.tile([P, 32], F32)
-        nc.vector.tensor_copy(out=z_cols[:], in_=z_acc[:, 0:32])
-        z_tot = psum.tile([P, 512], F32, tag="o")
-        nc.tensor.matmul(out=z_tot[:, 0:32], lhsT=ones_f[:], rhs=z_cols[:], start=True, stop=True)
-        zs = const.tile([P, 32], F32)
-        nc.vector.tensor_scalar(
-            out=zs[:], in0=z_tot[:, 0:32], scalar1=1.0 / BLOCK_ELEMS, scalar2=None, op0=ALU.mult
+        ident_f = const.tile([P, P], F32)
+        make_identity(nc, ident_f[:])
+        perm_f = const.tile([P, P], F32)
+        nc.vector.tensor_copy(
+            out=perm_f[:].rearrange("i (h v lam d) -> i h v lam d", h=2, v=2, d=2),
+            in_=ident_f[:].rearrange("i (h lam v d) -> i h v lam d", h=2, v=2, d=2),
         )
-        z_words = z_sb[:].bitcast(F32)
-        z_grouped = const.tile([P, NK * 2048], BF16, align_bytes=64)
-        for pj in range(NP * NJ):
-            p, j = pj // NJ, pj % NJ
-            zt = psum.tile([P, 512], F32, tag="xt")
-            for u in range(2):
-                for kh in range(2):
-                    first = (pj * 2 + kh) * 256 + u * P
-                    nc.tensor.transpose(
-                        zt[:, (u * 2 + kh) * P : (u * 2 + kh + 1) * P], z_words[:, first : first + P], perm_f[:]
-                    )
-            nc.scalar.activation(
-                out=z_grouped[:].rearrange("q (k j v p x u e) -> q k j v p x u e", k=NK, j=NJ, v=2, p=NP, x=32, u=2)[
-                    :, :, j, :, p, :, :, :
-                ],
-                in_=zt[:].bitcast(BF16).rearrange("q (u k v x e) -> q k v x u e", u=2, k=NK, v=2, x=32),
-                func=ACT.Sign,
-            )
-            for k in range(NK):
-                z_part = z_grouped[:].rearrange("q (k j v p y) -> q k j v p y", k=NK, j=NJ, v=2, p=NP)[:, k, j, :, p, :]
-                nc.vector.tensor_scalar(
-                    out=z_part,
-                    in0=z_part,
-                    scalar1=zs[:, pj * NK + k : pj * NK + k + 1],
-                    scalar2=None,
-                    op0=ALU.mult,
-                )
-        z_codes = const.tile([P, NK * 512], U32, align_bytes=64)
-        z_scales = const.tile([P, NK * 512], U8, align_bytes=64)
-        for k in range(NK):
-            nc.vector.quantize_mx(
-                out=z_codes[:, k * 512 : (k + 1) * 512].bitcast(FP8X4),
-                scales=z_scales[:, k * 512 : (k + 1) * 512],
-                in_=z_grouped[:, k * 2048 : (k + 1) * 2048],
-            )
-
-        def quantise_x(bt):
-            x_words = x_sb[bt][:].bitcast(F32)
-            x_grouped = work.tile([P, NK * P * 4], BF16, align_bytes=64)
-            x_grouped_words = x_grouped[:].bitcast(F32)
-            for kh in range(2):
-                xt = psum.tile([P, 512], F32, tag="xt")
-                for s in range(4):
-                    first = kh * 512 + s * P
-                    nc.tensor.transpose(xt[:, s * P : (s + 1) * P], x_words[:, first : first + P], ident_f[:])
-                nc.vector.tensor_copy(
-                    out=x_grouped_words[:, kh * 512 : (kh + 1) * 512].rearrange("q (kk b u) -> q kk b u", kk=2, u=2),
-                    in_=xt[:].rearrange("q (kk u b) -> q kk b u", kk=2, u=2),
-                )
-            x_codes = work.tile([P, NK * P], U32, align_bytes=64, bufs=3)
-            x_scales = work.tile([P, NK * P], U8, align_bytes=64, bufs=3)
-            nc.vector.quantize_mx(out=x_codes[:].bitcast(FP8X4), scales=x_scales[:], in_=x_grouped[:])
-            return x_codes, x_scales
-
-        x_ready = {0: quantise_x(0), 1: quantise_x(1)}
-
-        y_acc = psum.tile([P, 512], F32, tag="o")
-        for j in range(NJ):
-            mag = work.tile([P, 4 * N], BF16, tag="mag")
-            nc.vector.tensor_scalar(
-                out=mag[:].bitcast(I32),
-                in0=y_sb[:, j * 2048 : (j + 1) * 2048].bitcast(I32),
-                scalar1=CLEAR_SIGNS,
-                scalar2=None,
-                op0=ALU.bitwise_and,
-            )
-            for s in range(16):
-                nc.tensor.matmul(
-                    out=y_acc[:, 0:16],
-                    lhsT=mag[:, s * P : (s + 1) * P],
-                    rhs=pick_all[:, (j * NK + s % NK) * 16 : (j * NK + s % NK + 1) * 16],
-                    start=(j == 0 and s == 0),
-                    stop=(j == NJ - 1 and s == 15),
-                )
-        y_cols = const.tile([P, 16], F32)
-        nc.vector.tensor_copy(out=y_cols[:], in_=y_acc[:, 0:16])
-        y_tot = psum.tile([P, 512], F32, tag="o")
-        for p in range(NP):
-            nc.tensor.matmul(
-                out=y_tot[:, p * 16 : (p + 1) * 16],
-                lhsT=half_mask[:, p * P : (p + 1) * P],
-                rhs=y_cols[:],
-                start=True,
-                stop=True,
-            )
-        gain = const.tile([P, 32], F32)
-        nc.vector.scalar_tensor_tensor(
-            out=gain[:], in0=y_tot[:, 0:32], scalar=1.0 / BLOCK_ELEMS, in1=a_all[:], op0=ALU.mult, op1=ALU.mult
+        ones_f = const.tile([P, P], F32)
+        nc.vector.memset(ones_f[:], 1.0)
+        pick_half = const.tile([P, 16 * 32], BF16)
+        nc.vector.memset(pick_half[:], 0.0)
+        nc.vector.memset(pick_half[0:64, 0 : 16 * 32 : 34], 1.0)
+        nc.vector.memset(pick_half[64:P, 1 : 16 * 32 : 34], 1.0)
+        pick_all = const.tile([P, NK * 16], BF16)
+        nc.vector.memset(pick_all[:], 0.0)
+        nc.vector.memset(pick_all[:, 0 : NK * 16 : 17], 1.0)
+        same_p = const.tile([P, P], F32)
+        nc.vector.memset(same_p[:], 0.0)
+        nc.vector.memset(same_p[0:64, :].rearrange("r (k p lam) -> r k p lam", k=NK, p=NP)[:, :, 0, :], 1.0)
+        nc.vector.memset(same_p[64:P, :].rearrange("r (k p lam) -> r k p lam", k=NK, p=NP)[:, :, 1, :], 1.0)
+        group_of = const.tile([P, 8], F32)
+        nc.vector.tensor_reduce(
+            out=group_of[:], in_=ident_f[:].rearrange("q (g lam) -> q g lam", g=8), axis=AX.X, op=ALU.add
         )
-        own_gain = const.tile([P, 32], F32)
+        a_pick = const.tile([P, 32], F32)
         nc.vector.tensor_tensor(
-            out=own_gain[:].rearrange("q (j k p) -> q j k p", j=NJ, k=NK),
-            in0=gain[:].rearrange("q (p j k) -> q j k p", p=NP, j=NJ),
+            out=a_pick[:].rearrange("q (j k p) -> q j k p", j=NJ, k=NK),
+            in0=a_all[:].rearrange("q (p j k) -> q j k p", p=NP, j=NJ),
             in1=group_of[:].rearrange("q (k p) -> q k p", k=NK).unsqueeze(1).to_broadcast([P, NJ, NK, NP]),
             op=ALU.mult,
         )
-        w_gain = const.tile([P, NJ], F32)
+        a_own = const.tile([P, NJ * NK], F32)
         nc.vector.tensor_reduce(
-            out=w_gain[:], in_=own_gain[:].rearrange("q (j g) -> q j g", j=NJ), axis=AX.X, op=ALU.add
+            out=a_own[:], in_=a_pick[:].rearrange("q (jk p) -> q jk p", p=NP), axis=AX.X, op=ALU.add
         )
+
+        z_words = z_sb[:].bitcast(F32)
+        z_grouped = const.tile([P, NK * 2048], BF16, align_bytes=64)
+        z_codes = const.tile([P, NK * 512], U32, align_bytes=64)
+        z_scales = const.tile([P, NK * 512], U8, align_bytes=64)
+        zs = const.tile([P, 32], F32)
         y_words = y_sb[:].bitcast(F32)
         w_grouped = const.tile([P, NJ * 2048], BF16, align_bytes=64)
         w_codes = const.tile([P, NJ * 512], U32, align_bytes=64)
         w_scales = const.tile([P, NJ * 512], U8, align_bytes=64)
-        for j in range(NJ):
-            for mh in range(2):
-                yt = psum.tile([P, 512], F32, tag="xt")
-                for u in range(2):
-                    for mcc in range(2):
-                        first = (j * 4 + mh * 2 + mcc) * 256
-                        nc.tensor.transpose(
-                            yt[:, (u * 2 + mcc) * P : (u * 2 + mcc + 1) * P],
-                            y_words[:, first + u : first + 256 : 2],
-                            ident_f[:],
-                        )
-                nc.scalar.activation(
-                    out=w_grouped[:, (j * 2 + mh) * 1024 : (j * 2 + mh + 1) * 1024].rearrange(
-                        "q (m u e) -> q m u e", u=2, e=2
-                    ),
-                    in_=yt[:].bitcast(BF16).rearrange("q (u m e) -> q m u e", u=2, e=2),
-                    func=ACT.Sign,
-                )
+        w_gain = const.tile([P, NJ], F32)
+        mag = {}
+        col_sums = {}
+        col_sums_sb = {}
+        block_sums = {}
+
+        def magnitudes(s):
+            src = z_sb[:, s * 2048 : (s + 1) * 2048] if s < 4 else y_sb[:, (s - 4) * 2048 : (s - 3) * 2048]
+            mag[s] = work.tile([P, 2048], BF16, tag="mag", name="mag", bufs=3)
             nc.vector.tensor_scalar(
-                out=w_grouped[:, j * 2048 : (j + 1) * 2048],
-                in0=w_grouped[:, j * 2048 : (j + 1) * 2048],
-                scalar1=w_gain[:, j : j + 1],
-                scalar2=None,
-                op0=ALU.mult,
-            )
-            nc.vector.quantize_mx(
-                out=w_codes[:, j * 512 : (j + 1) * 512].bitcast(FP8X4),
-                scales=w_scales[:, j * 512 : (j + 1) * 512],
-                in_=w_grouped[:, j * 2048 : (j + 1) * 2048],
+                out=mag[s][:].bitcast(I32), in0=src.bitcast(I32), scalar1=CLEAR_SIGNS, scalar2=None, op0=ALU.bitwise_and
             )
 
-        for bt in range(B_TILES):
-            x_codes, x_scales = x_ready[bt]
-            t_rows = work.tile([P, 2048], BF16)
-            t_rows_view = t_rows[:].rearrange("b (jv k y) -> b jv k y", jv=8, k=NK)
-            t_words = t_rows[:].bitcast(F32)
-            for k in range(NK):
-                t_ps = psum.tile([P, 512], F32, tag="t")
-                nc.tensor.matmul_mx(
-                    out=t_ps[:],
-                    lhsT=x_codes[:, k * P : (k + 1) * P].bitcast(FP8X4),
-                    lhsT_scale=x_scales[:, k * P : (k + 1) * P],
-                    rhs=z_codes[:, k * 512 : (k + 1) * 512].bitcast(FP8X4),
-                    rhs_scale=z_scales[:, k * 512 : (k + 1) * 512],
-                    start=True,
-                    stop=True,
-                )
-                nc.scalar.copy(out=t_rows_view[:, :, k, :], in_=t_ps[:].rearrange("b (jv y) -> b jv y", jv=8))
-            if bt + 2 < B_TILES:
-                x_ready[bt + 2] = quantise_x(bt + 2)
-            t_grouped = work.tile([P, 2048], BF16, align_bytes=64)
-            t_grouped_words = t_grouped[:].bitcast(F32)
-            for jh in range(2):
-                tt = psum.tile([P, 512], F32, tag="tt")
-                for s in range(4):
-                    first = (jh * 4 + s) * P
-                    nc.tensor.transpose(tt[:, s * P : (s + 1) * P], t_words[:, first : first + P], ident_f[:])
-                nc.vector.tensor_copy(
-                    out=t_grouped_words[:, jh * 512 : (jh + 1) * 512].rearrange("q (jj b v) -> q jj b v", jj=2, v=2),
-                    in_=tt[:].rearrange("q (jj v b) -> q jj b v", jj=2, v=2),
-                )
-            t_codes = work.tile([P, NJ * P], U32, align_bytes=64)
-            t_scales = work.tile([P, NJ * P], U8, align_bytes=64)
-            nc.vector.quantize_mx(out=t_codes[:].bitcast(FP8X4), scales=t_scales[:], in_=t_grouped[:])
-            o_sb = work.tile([P, NJ * M], F32, bufs=3)
-            for j in range(NJ):
-                o_ps = psum.tile([P, 512], F32, tag="o")
-                nc.tensor.matmul_mx(
-                    out=o_ps[:],
-                    lhsT=t_codes[:, j * P : (j + 1) * P].bitcast(FP8X4),
-                    lhsT_scale=t_scales[:, j * P : (j + 1) * P],
-                    rhs=w_codes[:, j * 512 : (j + 1) * 512].bitcast(FP8X4),
-                    rhs_scale=w_scales[:, j * 512 : (j + 1) * 512],
-                    start=True,
-                    stop=True,
-                )
-                if j == 0:
-                    nc.vector.tensor_copy(out=o_sb[:, j * M : (j + 1) * M], in_=o_ps[:])
+        def signs(s):
+            for half in range(2):
+                bank = psum.tile([P, 512], F32, tag="tr", name="bank_w")
+                if s < 4:
+                    pj = s * 2 + half
+                    for u in range(2):
+                        for kh in range(2):
+                            first = (pj * 2 + kh) * 256 + u * P
+                            nc.tensor.transpose(
+                                bank[:, (u * 2 + kh) * P : (u * 2 + kh + 1) * P],
+                                z_words[:, first : first + P],
+                                perm_f[:],
+                            )
+                    nc.scalar.activation(
+                        out=z_grouped[:].rearrange("q (k pj c u e) -> q k pj c u e", k=NK, pj=8, c=64, u=2)[
+                            :, :, pj, :, :, :
+                        ],
+                        in_=bank[:].bitcast(BF16).rearrange("q (u k c e) -> q k c u e", u=2, k=NK, c=64),
+                        func=ACT.Sign,
+                    )
                 else:
-                    nc.scalar.copy(out=o_sb[:, j * M : (j + 1) * M], in_=o_ps[:])
-            nc.sync.dma_start(out=out_rows[bt * P : (bt + 1) * P, :], in_=o_sb[:])
+                    j = s - 4
+                    for u in range(2):
+                        for mcc in range(2):
+                            first = (j * 4 + half * 2 + mcc) * 256
+                            nc.tensor.transpose(
+                                bank[:, (u * 2 + mcc) * P : (u * 2 + mcc + 1) * P],
+                                y_words[:, first + u : first + 256 : 2],
+                                ident_f[:],
+                            )
+                    nc.scalar.activation(
+                        out=w_grouped[:, (j * 2 + half) * 1024 : (j * 2 + half + 1) * 1024].rearrange(
+                            "q (m u e) -> q m u e", u=2, e=2
+                        ),
+                        in_=bank[:].bitcast(BF16).rearrange("q (u m e) -> q m u e", u=2, e=2),
+                        func=ACT.Sign,
+                    )
+
+        def column_sums(s):
+            col_sums[s] = psum.tile([P, 512], F32, tag="mx", name="col_sums")
+            for c in range(16):
+                if s < 4:
+                    i = s * 4 + c // 4
+                    nc.tensor.matmul(
+                        out=col_sums[s][:, 0:32],
+                        lhsT=mag[s][:, c * P : (c + 1) * P],
+                        rhs=pick_half[:, i * 32 : (i + 1) * 32],
+                        start=(c == 0),
+                        stop=(c == 15),
+                    )
+                else:
+                    nc.tensor.matmul(
+                        out=col_sums[s][:, 0:16],
+                        lhsT=mag[s][:, c * P : (c + 1) * P],
+                        rhs=pick_all[:, (c % NK) * 16 : (c % NK + 1) * 16],
+                        start=(c == 0),
+                        stop=(c == 15),
+                    )
+
+        def column_sums_out(s):
+            col_sums_sb[s] = work.tile([P, 32], F32, tag="col_sums_sb", name="col_sums_sb")
+            width = 32 if s < 4 else 16
+            nc.vector.tensor_copy(out=col_sums_sb[s][:, 0:width], in_=col_sums[s][:, 0:width])
+
+        def sum_blocks(s):
+            block_sums[s] = psum.tile([P, 512], F32, tag="mx", name="block_sums")
+            if s < 4:
+                nc.tensor.matmul(
+                    out=block_sums[s][:, 0:32], lhsT=ones_f[:], rhs=col_sums_sb[s][:, 0:32], start=True, stop=True
+                )
+            else:
+                nc.tensor.matmul(
+                    out=block_sums[s][:, 0:16], lhsT=same_p[:], rhs=col_sums_sb[s][:, 0:16], start=True, stop=True
+                )
+
+        def scales_of(s):
+            if s < 4:
+                nc.vector.tensor_scalar(
+                    out=zs[:, s * 8 : (s + 1) * 8],
+                    in0=block_sums[s][:, s * 8 : (s + 1) * 8],
+                    scalar1=1.0 / BLOCK_ELEMS,
+                    scalar2=None,
+                    op0=ALU.mult,
+                )
+            else:
+                j = s - 4
+                gain = work.tile([P, NK], F32, tag="gain")
+                nc.vector.scalar_tensor_tensor(
+                    out=gain[:],
+                    in0=block_sums[s][:, 0:NK],
+                    scalar=1.0 / BLOCK_ELEMS,
+                    in1=a_own[:, j * NK : (j + 1) * NK],
+                    op0=ALU.mult,
+                    op1=ALU.mult,
+                )
+                nc.vector.tensor_reduce(out=w_gain[:, j : j + 1], in_=gain[:], axis=AX.X, op=ALU.add)
+
+        def finish(s):
+            if s < 4:
+                for pj in range(s * 2, s * 2 + 2):
+                    for k in range(NK):
+                        z_part = z_grouped[:, (k * 8 + pj) * 256 : (k * 8 + pj + 1) * 256]
+                        nc.vector.tensor_scalar(
+                            out=z_part,
+                            in0=z_part,
+                            scalar1=zs[:, pj * NK + k : pj * NK + k + 1],
+                            scalar2=None,
+                            op0=ALU.mult,
+                        )
+                for k in range(NK):
+                    nc.vector.quantize_mx(
+                        out=z_codes[:, k * 512 + s * P : k * 512 + (s + 1) * P].bitcast(FP8X4),
+                        scales=z_scales[:, k * 512 + s * P : k * 512 + (s + 1) * P],
+                        in_=z_grouped[:, k * 2048 + s * 512 : k * 2048 + (s + 1) * 512],
+                    )
+            else:
+                j = s - 4
+                nc.vector.tensor_scalar(
+                    out=w_grouped[:, j * 2048 : (j + 1) * 2048],
+                    in0=w_grouped[:, j * 2048 : (j + 1) * 2048],
+                    scalar1=w_gain[:, j : j + 1],
+                    scalar2=None,
+                    op0=ALU.mult,
+                )
+                nc.vector.quantize_mx(
+                    out=w_codes[:, j * 512 : (j + 1) * 512].bitcast(FP8X4),
+                    scales=w_scales[:, j * 512 : (j + 1) * 512],
+                    in_=w_grouped[:, j * 2048 : (j + 1) * 2048],
+                )
+
+        x_codes = {}
+        x_scales = {}
+        t_rows = {}
+        t_codes = {}
+        t_scales = {}
+        o_sb = {}
+
+        def quantise_transposed(rows, codes, scales):
+            grouped = work.tile([P, 2048], BF16, align_bytes=64, tag="grouped", name="grouped", bufs=3)
+            grouped_words = grouped[:].bitcast(F32)
+            for half in range(2):
+                bank = psum.tile([P, 512], F32, tag="tr", name="bank_t")
+                for s in range(4):
+                    first = half * 512 + s * P
+                    nc.tensor.transpose(bank[:, s * P : (s + 1) * P], rows[:, first : first + P], ident_f[:])
+                dst = grouped_words[:, half * 512 : (half + 1) * 512].rearrange("q (c b w) -> q c b w", c=2, w=2)
+                src = bank[:].rearrange("q (c w b) -> q c b w", c=2, w=2)
+                if half == 0:
+                    nc.scalar.copy(out=dst, in_=src)
+                else:
+                    nc.vector.tensor_copy(out=dst, in_=src)
+            nc.vector.quantize_mx(out=codes[:].bitcast(FP8X4), scales=scales[:], in_=grouped[:])
+
+        def quantise_x(n):
+            x_codes[n] = work.tile([P, NK * P], U32, align_bytes=64, tag="x_codes", name="x_codes")
+            x_scales[n] = work.tile([P, NK * P], U8, align_bytes=64, tag="x_scales", name="x_scales")
+            quantise_transposed(x_sb[n][:].bitcast(F32), x_codes[n], x_scales[n])
+
+        def first_matmul(n, k):
+            if k == 0:
+                t_rows[n] = work.tile([P, 2048], BF16, tag="t_rows", name="t_rows")
+            t_ps = psum.tile([P, 512], F32, tag="mx")
+            nc.tensor.matmul_mx(
+                out=t_ps[:],
+                lhsT=x_codes[n][:, k * P : (k + 1) * P].bitcast(FP8X4),
+                lhsT_scale=x_scales[n][:, k * P : (k + 1) * P],
+                rhs=z_codes[:, k * 512 : (k + 1) * 512].bitcast(FP8X4),
+                rhs_scale=z_scales[:, k * 512 : (k + 1) * 512],
+                start=True,
+                stop=True,
+            )
+            dst = t_rows[n][:].rearrange("b (jv k p y) -> b jv k p y", jv=8, k=NK, p=NP)[:, :, k, :, :]
+            src = t_ps[:].rearrange("b (p jv y) -> b jv p y", p=NP, jv=8)
+            if k == NK - 1:
+                nc.vector.tensor_copy(out=dst, in_=src)
+            else:
+                nc.scalar.copy(out=dst, in_=src)
+
+        def quantise_t(n):
+            t_codes[n] = work.tile([P, NJ * P], U32, align_bytes=64, tag="t_codes", name="t_codes")
+            t_scales[n] = work.tile([P, NJ * P], U8, align_bytes=64, tag="t_scales", name="t_scales")
+            quantise_transposed(t_rows[n][:].bitcast(F32), t_codes[n], t_scales[n])
+
+        def second_matmul(n, j):
+            if j == 0:
+                o_sb[n] = work.tile([P, NJ * M], F32, tag="o_sb", name="o_sb", bufs=3)
+            o_ps = psum.tile([P, 512], F32, tag="mx")
+            nc.tensor.matmul_mx(
+                out=o_ps[:],
+                lhsT=t_codes[n][:, j * P : (j + 1) * P].bitcast(FP8X4),
+                lhsT_scale=t_scales[n][:, j * P : (j + 1) * P],
+                rhs=w_codes[:, j * 512 : (j + 1) * 512].bitcast(FP8X4),
+                rhs_scale=w_scales[:, j * 512 : (j + 1) * 512],
+                start=True,
+                stop=True,
+            )
+            if j % 2 == 0:
+                nc.scalar.copy(out=o_sb[n][:, j * M : (j + 1) * M], in_=o_ps[:])
+            else:
+                nc.vector.tensor_copy(out=o_sb[n][:, j * M : (j + 1) * M], in_=o_ps[:])
+            if j == NJ - 1:
+                nc.sync.dma_start(out=out_rows[n * P : (n + 1) * P, :], in_=o_sb[n][:])
+
+        def is_item(s):
+            return 0 <= s < PREP_ITEMS
+
+        def is_tile(n):
+            return 0 <= n < B_TILES
+
+        for step in range(PREP_ITEMS + B_TILES + 2):
+            if is_item(step):
+                magnitudes(step)
+            if is_item(step - 1):
+                column_sums_out(step - 1)
+            if is_item(step):
+                signs(step)
+            if is_item(step - 1):
+                sum_blocks(step - 1)
+            if is_item(step):
+                column_sums(step)
+            if is_item(step - 2):
+                finish(step - 2)
+            if is_item(step - 1):
+                scales_of(step - 1)
+            n = step - PREP_ITEMS
+            if is_tile(n):
+                quantise_x(n)
+            for j in range(NJ):
+                if is_tile(n - 2):
+                    second_matmul(n - 2, j)
+            if is_tile(n - 1):
+                quantise_t(n - 1)
+            for k in range(NK):
+                if is_tile(n):
+                    first_matmul(n, k)

@@ -21,6 +21,7 @@ B_TILES = B // P
 BLOCK_ELEMS = M * L
 CLEAR_SIGNS = 0x7FFF7FFF
 PREP_ITEMS = 8
+PICK_WIDTH = 96
 FLOPS = 2 * (2 * B * N * NP * NJ * NK * L)
 
 
@@ -67,13 +68,13 @@ def tile_bqqlinear_pa_kernel(tc, x_q, Y_fp, Z_fp, a_core, out):
         )
         ones_f = const.tile([P, P], F32)
         nc.vector.memset(ones_f[:], 1.0)
-        pick_half = const.tile([P, 16 * 32], BF16)
+        pick_half = const.tile([P, 16 * PICK_WIDTH], BF16)
         nc.vector.memset(pick_half[:], 0.0)
-        nc.vector.memset(pick_half[0:64, 0 : 16 * 32 : 34], 1.0)
-        nc.vector.memset(pick_half[64:P, 1 : 16 * 32 : 34], 1.0)
-        pick_all = const.tile([P, NK * 16], BF16)
+        nc.vector.memset(pick_half[0:64, 0 : 16 * PICK_WIDTH : PICK_WIDTH + 2], 1.0)
+        nc.vector.memset(pick_half[64:P, 1 : 16 * PICK_WIDTH : PICK_WIDTH + 2], 1.0)
+        pick_all = const.tile([P, NK * PICK_WIDTH], BF16)
         nc.vector.memset(pick_all[:], 0.0)
-        nc.vector.memset(pick_all[:, 0 : NK * 16 : 17], 1.0)
+        nc.vector.memset(pick_all[:, 0 : NK * PICK_WIDTH : PICK_WIDTH + 1], 1.0)
         same_p = const.tile([P, P], F32)
         nc.vector.memset(same_p[:], 0.0)
         nc.vector.memset(same_p[0:64, :].rearrange("r (k p lam) -> r k p lam", k=NK, p=NP)[:, :, 0, :], 1.0)
@@ -160,17 +161,17 @@ def tile_bqqlinear_pa_kernel(tc, x_q, Y_fp, Z_fp, a_core, out):
                 if s < 4:
                     i = s * 4 + c // 4
                     nc.tensor.matmul(
-                        out=col_sums[s][:, 0:32],
+                        out=col_sums[s][:, 0:PICK_WIDTH],
                         lhsT=mag[s][:, c * P : (c + 1) * P],
-                        rhs=pick_half[:, i * 32 : (i + 1) * 32],
+                        rhs=pick_half[:, i * PICK_WIDTH : (i + 1) * PICK_WIDTH],
                         start=(c == 0),
                         stop=(c == 15),
                     )
                 else:
                     nc.tensor.matmul(
-                        out=col_sums[s][:, 0:16],
+                        out=col_sums[s][:, 0:PICK_WIDTH],
                         lhsT=mag[s][:, c * P : (c + 1) * P],
-                        rhs=pick_all[:, (c % NK) * 16 : (c % NK + 1) * 16],
+                        rhs=pick_all[:, (c % NK) * PICK_WIDTH : (c % NK + 1) * PICK_WIDTH],
                         start=(c == 0),
                         stop=(c == 15),
                     )

@@ -21,7 +21,6 @@ B_TILES = B // P
 BLOCK_ELEMS = M * L
 CLEAR_SIGNS = 0x7FFF7FFF
 PREP_ITEMS = 8
-PICK_WIDTH = 96
 FLOPS = 2 * (2 * B * N * NP * NJ * NK * L)
 
 
@@ -34,7 +33,7 @@ def tile_bqqlinear_pa_kernel(tc, x_q, Y_fp, Z_fp, a_core, out):
     with ExitStack() as ctx:
         const = ctx.enter_context(tc.tile_pool(name="const", bufs=1))
         work = ctx.enter_context(tc.tile_pool(name="work", bufs=2))
-        psum = ctx.enter_context(tc.psum_pool(name="psum", bufs=4))
+        psum = ctx.enter_context(tc.psum_pool(name="psum", bufs=8))
         ctx.enter_context(tc.manual_schedule())
 
         a_all = const.tile([P, NP * NJ * NK], BF16)
@@ -68,13 +67,13 @@ def tile_bqqlinear_pa_kernel(tc, x_q, Y_fp, Z_fp, a_core, out):
         )
         ones_f = const.tile([P, P], F32)
         nc.vector.memset(ones_f[:], 1.0)
-        pick_half = const.tile([P, 16 * PICK_WIDTH], BF16)
+        pick_half = const.tile([P, 16 * 32], BF16)
         nc.vector.memset(pick_half[:], 0.0)
-        nc.vector.memset(pick_half[0:64, 0 : 16 * PICK_WIDTH : PICK_WIDTH + 2], 1.0)
-        nc.vector.memset(pick_half[64:P, 1 : 16 * PICK_WIDTH : PICK_WIDTH + 2], 1.0)
-        pick_all = const.tile([P, NK * PICK_WIDTH], BF16)
+        nc.vector.memset(pick_half[0:64, 0 : 16 * 32 : 34], 1.0)
+        nc.vector.memset(pick_half[64:P, 1 : 16 * 32 : 34], 1.0)
+        pick_all = const.tile([P, NK * 16], BF16)
         nc.vector.memset(pick_all[:], 0.0)
-        nc.vector.memset(pick_all[:, 0 : NK * PICK_WIDTH : PICK_WIDTH + 1], 1.0)
+        nc.vector.memset(pick_all[:, 0 : NK * 16 : 17], 1.0)
         same_p = const.tile([P, P], F32)
         nc.vector.memset(same_p[:], 0.0)
         nc.vector.memset(same_p[0:64, :].rearrange("r (k p lam) -> r k p lam", k=NK, p=NP)[:, :, 0, :], 1.0)
@@ -119,7 +118,7 @@ def tile_bqqlinear_pa_kernel(tc, x_q, Y_fp, Z_fp, a_core, out):
 
         def signs(s):
             for half in range(2):
-                bank = psum.tile([P, 512], F32, tag="tr", name="bank_w")
+                bank = psum.tile([P, 512], F32, tag="bank", name="bank_w")
                 if s < 4:
                     pj = s * 2 + half
                     for u in range(2):
@@ -156,22 +155,22 @@ def tile_bqqlinear_pa_kernel(tc, x_q, Y_fp, Z_fp, a_core, out):
                     )
 
         def column_sums(s):
-            col_sums[s] = psum.tile([P, 512], F32, tag="mx", name="col_sums")
+            col_sums[s] = psum.tile([P, 512], F32, tag="bank", name="col_sums")
             for c in range(16):
                 if s < 4:
                     i = s * 4 + c // 4
                     nc.tensor.matmul(
-                        out=col_sums[s][:, 0:PICK_WIDTH],
+                        out=col_sums[s][:, 0:32],
                         lhsT=mag[s][:, c * P : (c + 1) * P],
-                        rhs=pick_half[:, i * PICK_WIDTH : (i + 1) * PICK_WIDTH],
+                        rhs=pick_half[:, i * 32 : (i + 1) * 32],
                         start=(c == 0),
                         stop=(c == 15),
                     )
                 else:
                     nc.tensor.matmul(
-                        out=col_sums[s][:, 0:PICK_WIDTH],
+                        out=col_sums[s][:, 0:16],
                         lhsT=mag[s][:, c * P : (c + 1) * P],
-                        rhs=pick_all[:, (c % NK) * PICK_WIDTH : (c % NK + 1) * PICK_WIDTH],
+                        rhs=pick_all[:, (c % NK) * 16 : (c % NK + 1) * 16],
                         start=(c == 0),
                         stop=(c == 15),
                     )
@@ -182,7 +181,7 @@ def tile_bqqlinear_pa_kernel(tc, x_q, Y_fp, Z_fp, a_core, out):
             nc.vector.tensor_copy(out=col_sums_sb[s][:, 0:width], in_=col_sums[s][:, 0:width])
 
         def sum_blocks(s):
-            block_sums[s] = psum.tile([P, 512], F32, tag="mx", name="block_sums")
+            block_sums[s] = psum.tile([P, 512], F32, tag="bank", name="block_sums")
             if s < 4:
                 nc.tensor.matmul(
                     out=block_sums[s][:, 0:32], lhsT=ones_f[:], rhs=col_sums_sb[s][:, 0:32], start=True, stop=True
@@ -258,27 +257,25 @@ def tile_bqqlinear_pa_kernel(tc, x_q, Y_fp, Z_fp, a_core, out):
             grouped = work.tile([P, 2048], BF16, align_bytes=64, tag="grouped", name="grouped", bufs=3)
             grouped_words = grouped[:].bitcast(F32)
             for half in range(2):
-                bank = psum.tile([P, 512], F32, tag="tr", name="bank_t")
+                bank = psum.tile([P, 512], F32, tag="bank", name="bank_t")
                 for s in range(4):
                     first = half * 512 + s * P
                     nc.tensor.transpose(bank[:, s * P : (s + 1) * P], rows[:, first : first + P], ident_f[:])
-                dst = grouped_words[:, half * 512 : (half + 1) * 512].rearrange("q (c b w) -> q c b w", c=2, w=2)
-                src = bank[:].rearrange("q (c w b) -> q c b w", c=2, w=2)
-                if half == 0:
-                    nc.scalar.copy(out=dst, in_=src)
-                else:
-                    nc.vector.tensor_copy(out=dst, in_=src)
+                nc.vector.tensor_copy(
+                    out=grouped_words[:, half * 512 : (half + 1) * 512].rearrange("q (c b w) -> q c b w", c=2, w=2),
+                    in_=bank[:].rearrange("q (c w b) -> q c b w", c=2, w=2),
+                )
             nc.vector.quantize_mx(out=codes[:].bitcast(FP8X4), scales=scales[:], in_=grouped[:])
 
         def quantise_x(n):
-            x_codes[n] = work.tile([P, NK * P], U32, align_bytes=64, tag="x_codes", name="x_codes")
-            x_scales[n] = work.tile([P, NK * P], U8, align_bytes=64, tag="x_scales", name="x_scales")
+            x_codes[n] = work.tile([P, NK * P], U32, align_bytes=64, tag="x_codes", name="x_codes", bufs=3)
+            x_scales[n] = work.tile([P, NK * P], U8, align_bytes=64, tag="x_scales", name="x_scales", bufs=3)
             quantise_transposed(x_sb[n][:].bitcast(F32), x_codes[n], x_scales[n])
 
         def first_matmul(n, k):
             if k == 0:
-                t_rows[n] = work.tile([P, 2048], BF16, tag="t_rows", name="t_rows")
-            t_ps = psum.tile([P, 512], F32, tag="mx")
+                t_rows[n] = work.tile([P, 2048], BF16, tag="t_rows", name="t_rows", bufs=3)
+            t_ps = psum.tile([P, 512], F32, tag="bank")
             nc.tensor.matmul_mx(
                 out=t_ps[:],
                 lhsT=x_codes[n][:, k * P : (k + 1) * P].bitcast(FP8X4),
@@ -288,22 +285,20 @@ def tile_bqqlinear_pa_kernel(tc, x_q, Y_fp, Z_fp, a_core, out):
                 start=True,
                 stop=True,
             )
-            dst = t_rows[n][:].rearrange("b (jv k p y) -> b jv k p y", jv=8, k=NK, p=NP)[:, :, k, :, :]
-            src = t_ps[:].rearrange("b (p jv y) -> b jv p y", p=NP, jv=8)
-            if k == NK - 1:
-                nc.vector.tensor_copy(out=dst, in_=src)
-            else:
-                nc.scalar.copy(out=dst, in_=src)
+            nc.scalar.copy(
+                out=t_rows[n][:].rearrange("b (jv k p y) -> b jv k p y", jv=8, k=NK, p=NP)[:, :, k, :, :],
+                in_=t_ps[:].rearrange("b (p jv y) -> b jv p y", p=NP, jv=8),
+            )
 
         def quantise_t(n):
-            t_codes[n] = work.tile([P, NJ * P], U32, align_bytes=64, tag="t_codes", name="t_codes")
-            t_scales[n] = work.tile([P, NJ * P], U8, align_bytes=64, tag="t_scales", name="t_scales")
+            t_codes[n] = work.tile([P, NJ * P], U32, align_bytes=64, tag="t_codes", name="t_codes", bufs=4)
+            t_scales[n] = work.tile([P, NJ * P], U8, align_bytes=64, tag="t_scales", name="t_scales", bufs=4)
             quantise_transposed(t_rows[n][:].bitcast(F32), t_codes[n], t_scales[n])
 
         def second_matmul(n, j):
             if j == 0:
                 o_sb[n] = work.tile([P, NJ * M], F32, tag="o_sb", name="o_sb", bufs=3)
-            o_ps = psum.tile([P, 512], F32, tag="mx")
+            o_ps = psum.tile([P, 512], F32, tag="bank")
             nc.tensor.matmul_mx(
                 out=o_ps[:],
                 lhsT=t_codes[n][:, j * P : (j + 1) * P].bitcast(FP8X4),
@@ -313,12 +308,11 @@ def tile_bqqlinear_pa_kernel(tc, x_q, Y_fp, Z_fp, a_core, out):
                 start=True,
                 stop=True,
             )
-            if j % 2 == 0:
-                nc.scalar.copy(out=o_sb[n][:, j * M : (j + 1) * M], in_=o_ps[:])
-            else:
-                nc.vector.tensor_copy(out=o_sb[n][:, j * M : (j + 1) * M], in_=o_ps[:])
             if j == NJ - 1:
-                nc.sync.dma_start(out=out_rows[n * P : (n + 1) * P, :], in_=o_sb[n][:])
+                nc.vector.tensor_copy(out=o_sb[n][:, j * M : (j + 1) * M], in_=o_ps[:])
+            else:
+                nc.scalar.copy(out=o_sb[n][:, j * M : (j + 1) * M], in_=o_ps[:])
+            nc.sync.dma_start(out=out_rows[n * P : (n + 1) * P, j * M : (j + 1) * M], in_=o_sb[n][:, j * M : (j + 1) * M])
 
         def is_item(s):
             return 0 <= s < PREP_ITEMS
@@ -326,29 +320,27 @@ def tile_bqqlinear_pa_kernel(tc, x_q, Y_fp, Z_fp, a_core, out):
         def is_tile(n):
             return 0 <= n < B_TILES
 
-        for step in range(PREP_ITEMS + B_TILES + 2):
+        for step in range(PREP_ITEMS + B_TILES + 3):
             if is_item(step):
                 magnitudes(step)
             if is_item(step - 1):
                 column_sums_out(step - 1)
             if is_item(step):
                 signs(step)
+                column_sums(step)
             if is_item(step - 1):
                 sum_blocks(step - 1)
-            if is_item(step):
-                column_sums(step)
             if is_item(step - 2):
+                scales_of(step - 2)
                 finish(step - 2)
-            if is_item(step - 1):
-                scales_of(step - 1)
             n = step - PREP_ITEMS
-            if is_tile(n):
-                quantise_x(n)
             for j in range(NJ):
-                if is_tile(n - 2):
-                    second_matmul(n - 2, j)
-            if is_tile(n - 1):
-                quantise_t(n - 1)
+                if is_tile(n - 3):
+                    second_matmul(n - 3, j)
+            if is_tile(n + 1):
+                quantise_x(n + 1)
             for k in range(NK):
                 if is_tile(n):
                     first_matmul(n, k)
+            if is_tile(n - 1):
+                quantise_t(n - 1)

@@ -233,18 +233,20 @@ def tile_bqqlinear_pa_kernel(tc, x_q, Y_fp, Z_fp, a_core, out):
                     )
             else:
                 j = s - 4
-                nc.vector.tensor_scalar(
-                    out=w_grouped[:, j * 2048 : (j + 1) * 2048],
-                    in0=w_grouped[:, j * 2048 : (j + 1) * 2048],
-                    scalar1=w_gain[:, j : j + 1],
-                    scalar2=None,
-                    op0=ALU.mult,
-                )
-                nc.vector.quantize_mx(
-                    out=w_codes[:, j * 512 : (j + 1) * 512].bitcast(FP8X4),
-                    scales=w_scales[:, j * 512 : (j + 1) * 512],
-                    in_=w_grouped[:, j * 2048 : (j + 1) * 2048],
-                )
+                for h in range(j * 2, j * 2 + 2):
+                    nc.vector.tensor_scalar(
+                        out=w_grouped[:, h * 1024 : (h + 1) * 1024],
+                        in0=w_grouped[:, h * 1024 : (h + 1) * 1024],
+                        scalar1=w_gain[:, j : j + 1],
+                        scalar2=None,
+                        op0=ALU.mult,
+                    )
+                for h in range(j * 2, j * 2 + 2):
+                    nc.vector.quantize_mx(
+                        out=w_codes[:, h * 256 : (h + 1) * 256].bitcast(FP8X4),
+                        scales=w_scales[:, h * 256 : (h + 1) * 256],
+                        in_=w_grouped[:, h * 1024 : (h + 1) * 1024],
+                    )
 
         x_codes = {}
         x_scales = {}
@@ -265,7 +267,12 @@ def tile_bqqlinear_pa_kernel(tc, x_q, Y_fp, Z_fp, a_core, out):
                     out=grouped_words[:, half * 512 : (half + 1) * 512].rearrange("q (c b w) -> q c b w", c=2, w=2),
                     in_=bank[:].rearrange("q (c w b) -> q c b w", c=2, w=2),
                 )
-            nc.vector.quantize_mx(out=codes[:].bitcast(FP8X4), scales=scales[:], in_=grouped[:])
+            for half in range(2):
+                nc.vector.quantize_mx(
+                    out=codes[:, half * 256 : (half + 1) * 256].bitcast(FP8X4),
+                    scales=scales[:, half * 256 : (half + 1) * 256],
+                    in_=grouped[:, half * 1024 : (half + 1) * 1024],
+                )
 
         def quantise_x(n):
             x_codes[n] = work.tile([P, NK * P], U32, align_bytes=64, tag="x_codes", name="x_codes", bufs=3)

@@ -7,9 +7,7 @@ BF16 = mybir.dt.bfloat16
 F32 = mybir.dt.float32
 U32 = mybir.dt.uint32
 U8 = mybir.dt.uint8
-I32 = mybir.dt.int32
 FP8X4 = mybir.dt.float8_e4m3fn_x4
-ACT = mybir.ActivationFunctionType
 ALU = mybir.AluOpType
 AX = mybir.AxisListType
 
@@ -19,8 +17,9 @@ M, L, N = 512, 64, 512
 B = 1024
 B_TILES = B // P
 BLOCK_ELEMS = M * L
-CLEAR_SIGNS = 0x7FFF7FFF
-PREP_ITEMS = 8
+TINY = 2.0**-100
+Z_ITEMS = 4
+ITEMS = Z_ITEMS + NJ
 FLOPS = 2 * (2 * B * N * NP * NJ * NK * L)
 
 
@@ -28,7 +27,7 @@ def tile_bqqlinear_pa_kernel(tc, x_q, Y_fp, Z_fp, a_core, out):
     nc = tc.nc
     x_rows = x_q.flatten_outer_dims()
     out_rows = out.rearrange("b j m -> b (j m)")
-    z_tiles = Z_fp.rearrange("p j k l n -> (p j k l) n").rearrange("(i r) n -> r i n", r=P)
+    z_chunks = Z_fp.rearrange("p j k l n -> (p j k l) n").rearrange("(s r x) n -> s r (x n)", s=Z_ITEMS, r=P)
 
     with ExitStack() as ctx:
         const = ctx.enter_context(tc.tile_pool(name="const", bufs=1))
@@ -38,316 +37,349 @@ def tile_bqqlinear_pa_kernel(tc, x_q, Y_fp, Z_fp, a_core, out):
 
         a_all = const.tile([P, NP * NJ * NK], BF16)
         nc.scalar.dma_start(out=a_all[:], in_=a_core.rearrange("p j k -> (p j k)").partition_broadcast(P))
-        z_sb = const.tile([P, 16 * N], BF16)
-        for g in range(4):
-            nc.sync.dma_start(
-                out=z_sb[:, g * 4 * N : (g + 1) * 4 * N].rearrange("r (i n) -> r i n", n=N),
-                in_=z_tiles[:, g * 4 : (g + 1) * 4, :],
-            )
-        y_sb = const.tile([P, NJ * 4 * 8 * L], BF16)
-        y_view = y_sb[:].rearrange("r (j mc g l) -> r j mc g l", j=NJ, mc=4, g=8)
-        with nc.allow_non_contiguous_dma(reason="rows of 64 bfloat16 values"):
-            for j in range(NJ):
-                for k in range(NK):
+        raw = [const.tile([P, 2048], BF16, name="raw%d" % s) for s in range(ITEMS)]
+        x_sb = [const.tile([P, NK * N], BF16, name="x_sb%d" % n) for n in range(B_TILES)]
+
+        def load_item(s):
+            if s < Z_ITEMS:
+                nc.sync.dma_start(out=raw[s][:], in_=z_chunks[s])
+            else:
+                with nc.allow_non_contiguous_dma(reason="rows of four m, 256 bfloat16 values"):
                     for p in range(NP):
                         nc.sync.dma_start(
-                            out=y_view[:, j, :, k * NP + p, :],
-                            in_=Y_fp[p, j, k].rearrange("(mc r) l -> r mc l", r=P),
+                            out=raw[s][:, p * 1024 : (p + 1) * 1024].rearrange("r (k x) -> r k x", k=NK),
+                            in_=Y_fp[p, s - Z_ITEMS].rearrange("k (r mc) l -> r k (mc l)", mc=4),
                         )
-        x_sb = [const.tile([P, NK * N], BF16, name="x_sb%d" % n) for n in range(B_TILES)]
-        for n in range(B_TILES):
-            nc.sync.dma_start(out=x_sb[n][:], in_=x_rows[n * P : (n + 1) * P, :])
+
+        for s in range(ITEMS):
+            load_item(s)
+            nc.sync.dma_start(out=x_sb[s][:], in_=x_rows[s * P : (s + 1) * P, :])
 
         ident_f = const.tile([P, P], F32)
         make_identity(nc, ident_f[:])
-        perm_f = const.tile([P, P], F32)
-        nc.vector.tensor_copy(
-            out=perm_f[:].rearrange("i (h v lam d) -> i h v lam d", h=2, v=2, d=2),
-            in_=ident_f[:].rearrange("i (h lam v d) -> i h v lam d", h=2, v=2, d=2),
-        )
         ones_f = const.tile([P, P], F32)
         nc.vector.memset(ones_f[:], 1.0)
-        pick_half = const.tile([P, 16 * 32], BF16)
-        nc.vector.memset(pick_half[:], 0.0)
-        nc.vector.memset(pick_half[0:64, 0 : 16 * 32 : 34], 1.0)
-        nc.vector.memset(pick_half[64:P, 1 : 16 * 32 : 34], 1.0)
-        pick_all = const.tile([P, NK * 16], BF16)
-        nc.vector.memset(pick_all[:], 0.0)
-        nc.vector.memset(pick_all[:, 0 : NK * 16 : 17], 1.0)
-        same_p = const.tile([P, P], F32)
-        nc.vector.memset(same_p[:], 0.0)
-        nc.vector.memset(same_p[0:64, :].rearrange("r (k p lam) -> r k p lam", k=NK, p=NP)[:, :, 0, :], 1.0)
-        nc.vector.memset(same_p[64:P, :].rearrange("r (k p lam) -> r k p lam", k=NK, p=NP)[:, :, 1, :], 1.0)
-        group_of = const.tile([P, 8], F32)
+        pick_g = const.tile([P, 64], BF16)
+        nc.vector.memset(pick_g[:], 0.0)
+        nc.vector.memset(pick_g[:, 0:64:9], 1.0)
+        pick_h = const.tile([P, 4], BF16)
+        nc.vector.memset(pick_h[:], 0.0)
+        nc.vector.memset(pick_h[:, 0:4:3], 1.0)
+        same_g4 = const.tile([P, P], F32)
+        nc.vector.memset(same_g4[:], 0.0)
+        for i in range(4):
+            nc.vector.memset(
+                same_g4[32 * i : 32 * i + 32, :].rearrange("x (h g lam) -> x h g lam", h=2, g=4)[:, :, i, :], 1.0
+            )
+        own = const.tile([P, 10], F32)
         nc.vector.tensor_reduce(
-            out=group_of[:], in_=ident_f[:].rearrange("q (g lam) -> q g lam", g=8), axis=AX.X, op=ALU.add
+            out=own[:, 0:8], in_=ident_f[:].rearrange("q (g lam) -> q g lam", g=8), axis=AX.X, op=ALU.add
+        )
+        halves = const.tile([P, 2], F32)
+        nc.vector.tensor_reduce(
+            out=halves[:], in_=ident_f[:].rearrange("q (h x) -> q h x", h=2), axis=AX.X, op=ALU.add
         )
         a_pick = const.tile([P, 32], F32)
         nc.vector.tensor_tensor(
-            out=a_pick[:].rearrange("q (j k p) -> q j k p", j=NJ, k=NK),
-            in0=a_all[:].rearrange("q (p j k) -> q j k p", p=NP, j=NJ),
-            in1=group_of[:].rearrange("q (k p) -> q k p", k=NK).unsqueeze(1).to_broadcast([P, NJ, NK, NP]),
+            out=a_pick[:].rearrange("q (j p k) -> q j p k", j=NJ, p=NP),
+            in0=a_all[:].rearrange("q (p j k) -> q j p k", p=NP, j=NJ),
+            in1=own[:, 0:8].rearrange("q (p k) -> q p k", p=NP).unsqueeze(1).to_broadcast([P, NJ, NP, NK]),
             op=ALU.mult,
         )
-        a_own = const.tile([P, NJ * NK], F32)
+        pick_z = const.tile([P, 8], BF16)
+        nc.vector.tensor_copy(out=pick_z[:], in_=own[:, 0:8])
+        pick_z2 = const.tile([P, 8], BF16)
+        nc.vector.tensor_scalar(out=pick_z2[:], in0=own[:, 0:8], scalar1=-2.0, scalar2=None, op0=ALU.mult)
+        nc.vector.tensor_scalar(out=own[:, 8:10], in0=halves[:], scalar1=-2.0, scalar2=None, op0=ALU.mult)
+        a_sum = const.tile([P, NJ], F32)
         nc.vector.tensor_reduce(
-            out=a_own[:], in_=a_pick[:].rearrange("q (jk p) -> q jk p", p=NP), axis=AX.X, op=ALU.add
+            out=a_sum[:], in_=a_pick[:].rearrange("q (j g) -> q j g", j=NJ), axis=AX.X, op=ALU.add
+        )
+        a_own = const.tile([P, NJ], F32)
+        nc.vector.tensor_scalar(
+            out=a_own[:], in0=a_sum[:], scalar1=1.0 / (TINY * BLOCK_ELEMS), scalar2=None, op0=ALU.mult
         )
 
-        z_words = z_sb[:].bitcast(F32)
-        z_grouped = const.tile([P, NK * 2048], BF16, align_bytes=64)
+        z_grouped = [const.tile([P, 2048], BF16, align_bytes=64, name="z_grouped%d" % s) for s in range(Z_ITEMS)]
         z_codes = const.tile([P, NK * 512], U32, align_bytes=64)
         z_scales = const.tile([P, NK * 512], U8, align_bytes=64)
-        zs = const.tile([P, 32], F32)
-        y_words = y_sb[:].bitcast(F32)
         w_grouped = const.tile([P, NJ * 2048], BF16, align_bytes=64)
         w_codes = const.tile([P, NJ * 512], U32, align_bytes=64)
         w_scales = const.tile([P, NJ * 512], U8, align_bytes=64)
-        w_gain = const.tile([P, NJ], F32)
-        mag = {}
+        gain = const.tile([P, ITEMS], F32)
+        low = {}
         col_sums = {}
         col_sums_sb = {}
         block_sums = {}
+        banks = {}
 
-        def magnitudes(s):
-            src = z_sb[:, s * 2048 : (s + 1) * 2048] if s < 4 else y_sb[:, (s - 4) * 2048 : (s - 3) * 2048]
-            mag[s] = work.tile([P, 2048], BF16, tag="mag", name="mag", bufs=3)
-            nc.vector.tensor_scalar(
-                out=mag[s][:].bitcast(I32), in0=src.bitcast(I32), scalar1=CLEAR_SIGNS, scalar2=None, op0=ALU.bitwise_and
-            )
+        def clamp_above(s):
+            low[s] = work.tile([P, 2048], BF16, tag="low", name="low", bufs=4)
+            if s < Z_ITEMS:
+                o, i = low[s][:], raw[s][:]
+            else:
+                o = low[s][:].rearrange("r (mw g y) -> r mw g y", mw=8, g=8)
+                i = raw[s][:].rearrange("r (g mw y) -> r mw g y", mw=8, g=8)
+            nc.vector.tensor_scalar(out=o, in0=i, scalar1=TINY, scalar2=None, op0=ALU.min)
 
-        def signs(s):
-            for half in range(2):
-                bank = psum.tile([P, 512], F32, tag="bank", name="bank_w")
-                if s < 4:
-                    pj = s * 2 + half
-                    for u in range(2):
-                        for kh in range(2):
-                            first = (pj * 2 + kh) * 256 + u * P
-                            nc.tensor.transpose(
-                                bank[:, (u * 2 + kh) * P : (u * 2 + kh + 1) * P],
-                                z_words[:, first : first + P],
-                                perm_f[:],
-                            )
-                    nc.scalar.activation(
-                        out=z_grouped[:].rearrange("q (k pj c u e) -> q k pj c u e", k=NK, pj=8, c=64, u=2)[
-                            :, :, pj, :, :, :
-                        ],
-                        in_=bank[:].bitcast(BF16).rearrange("q (u k c e) -> q k c u e", u=2, k=NK, c=64),
-                        func=ACT.Sign,
-                    )
-                else:
-                    j = s - 4
-                    for u in range(2):
-                        for mcc in range(2):
-                            first = (j * 4 + half * 2 + mcc) * 256
-                            nc.tensor.transpose(
-                                bank[:, (u * 2 + mcc) * P : (u * 2 + mcc + 1) * P],
-                                y_words[:, first + u : first + 256 : 2],
-                                ident_f[:],
-                            )
-                    nc.scalar.activation(
-                        out=w_grouped[:, (j * 2 + half) * 1024 : (j * 2 + half + 1) * 1024].rearrange(
-                            "q (m u e) -> q m u e", u=2, e=2
-                        ),
-                        in_=bank[:].bitcast(BF16).rearrange("q (u m e) -> q m u e", u=2, e=2),
-                        func=ACT.Sign,
-                    )
-
-        def column_sums(s):
+        def sums_raw(s):
             col_sums[s] = psum.tile([P, 512], F32, tag="bank", name="col_sums")
             for c in range(16):
-                if s < 4:
-                    i = s * 4 + c // 4
+                if s < Z_ITEMS:
                     nc.tensor.matmul(
-                        out=col_sums[s][:, 0:32],
-                        lhsT=mag[s][:, c * P : (c + 1) * P],
-                        rhs=pick_half[:, i * 32 : (i + 1) * 32],
-                        start=(c == 0),
-                        stop=(c == 15),
+                        out=col_sums[s][:, 0:8], lhsT=raw[s][:, c * P : (c + 1) * P], rhs=pick_z[:], start=(c == 0), stop=False
                     )
                 else:
+                    g = c // 2
                     nc.tensor.matmul(
-                        out=col_sums[s][:, 0:16],
-                        lhsT=mag[s][:, c * P : (c + 1) * P],
-                        rhs=pick_all[:, (c % NK) * 16 : (c % NK + 1) * 16],
+                        out=col_sums[s][:, 0:8],
+                        lhsT=raw[s][:, c * P : (c + 1) * P],
+                        rhs=pick_g[:, g * 8 : (g + 1) * 8],
                         start=(c == 0),
                         stop=(c == 15),
                     )
 
-        def column_sums_out(s):
-            col_sums_sb[s] = work.tile([P, 32], F32, tag="col_sums_sb", name="col_sums_sb")
-            width = 32 if s < 4 else 16
-            nc.vector.tensor_copy(out=col_sums_sb[s][:, 0:width], in_=col_sums[s][:, 0:width])
+        def sums_low(s):
+            for c in range(16):
+                if s < Z_ITEMS:
+                    nc.tensor.matmul(
+                        out=col_sums[s][:, 0:8], lhsT=low[s][:, c * P : (c + 1) * P], rhs=pick_z2[:], start=False, stop=(c == 15)
+                    )
+                else:
+                    h = c % 2
+                    nc.tensor.matmul(
+                        out=col_sums[s][:, 8:10],
+                        lhsT=low[s][:, c * P : (c + 1) * P],
+                        rhs=pick_h[:, h * 2 : (h + 1) * 2],
+                        start=(c == 0),
+                        stop=(c == 15),
+                    )
+
+        def sums_out(s):
+            col_sums_sb[s] = work.tile([P, 10], F32, tag="col_sums_sb", name="col_sums_sb")
+            width = 8 if s < Z_ITEMS else 10
+            nc.scalar.copy(out=col_sums_sb[s][:, 0:width], in_=col_sums[s][:, 0:width])
 
         def sum_blocks(s):
             block_sums[s] = psum.tile([P, 512], F32, tag="bank", name="block_sums")
-            if s < 4:
+            nc.tensor.matmul(
+                out=block_sums[s][:, 0:8], lhsT=ones_f[:], rhs=col_sums_sb[s][:, 0:8], start=True, stop=True
+            )
+            if s >= Z_ITEMS:
                 nc.tensor.matmul(
-                    out=block_sums[s][:, 0:32], lhsT=ones_f[:], rhs=col_sums_sb[s][:, 0:32], start=True, stop=True
-                )
-            else:
-                nc.tensor.matmul(
-                    out=block_sums[s][:, 0:16], lhsT=same_p[:], rhs=col_sums_sb[s][:, 0:16], start=True, stop=True
+                    out=block_sums[s][:, 8:10], lhsT=same_g4[:], rhs=col_sums_sb[s][:, 8:10], start=True, stop=True
                 )
 
-        def scales_of(s):
-            if s < 4:
-                nc.vector.tensor_scalar(
-                    out=zs[:, s * 8 : (s + 1) * 8],
-                    in0=block_sums[s][:, s * 8 : (s + 1) * 8],
-                    scalar1=1.0 / BLOCK_ELEMS,
-                    scalar2=None,
-                    op0=ALU.mult,
-                )
-            else:
-                j = s - 4
-                gain = work.tile([P, NK], F32, tag="gain")
-                nc.vector.scalar_tensor_tensor(
-                    out=gain[:],
-                    in0=block_sums[s][:, 0:NK],
-                    scalar=1.0 / BLOCK_ELEMS,
-                    in1=a_own[:, j * NK : (j + 1) * NK],
-                    op0=ALU.mult,
-                    op1=ALU.mult,
-                )
-                nc.vector.tensor_reduce(out=w_gain[:, j : j + 1], in_=gain[:], axis=AX.X, op=ALU.add)
+        def gain_of(s):
+            width = 8 if s < Z_ITEMS else 10
+            spare = work.tile([P, 10], F32, tag="spare", name="spare")
+            nc.vector.scalar_tensor_tensor(
+                out=spare[:, 0:width],
+                in0=block_sums[s][:, 0:width],
+                scalar=1.0 / (TINY * BLOCK_ELEMS) if s < Z_ITEMS else a_own[:, s - Z_ITEMS : s - Z_ITEMS + 1],
+                in1=own[:, 0:width],
+                op0=ALU.mult,
+                op1=ALU.mult,
+                accum_out=gain[:, s : s + 1],
+            )
 
-        def finish(s):
-            if s < 4:
-                for pj in range(s * 2, s * 2 + 2):
-                    for k in range(NK):
-                        z_part = z_grouped[:, (k * 8 + pj) * 256 : (k * 8 + pj + 1) * 256]
-                        nc.vector.tensor_scalar(
-                            out=z_part,
-                            in0=z_part,
-                            scalar1=zs[:, pj * NK + k : pj * NK + k + 1],
-                            scalar2=None,
-                            op0=ALU.mult,
-                        )
+        def scale(s):
+            part = low[s][:] if s < Z_ITEMS else w_grouped[:, (s - Z_ITEMS) * 2048 : (s - Z_ITEMS + 1) * 2048]
+            nc.vector.tensor_scalar(
+                out=part, in0=part, scalar1=-TINY, scalar2=gain[:, s : s + 1], op0=ALU.max, op1=ALU.mult
+            )
+
+        def transpose_item(s):
+            words = low[s][:].bitcast(F32)
+            for h in range(2):
+                banks[s, h] = psum.tile([P, 512], F32, tag="bank", name="bank_w")
+                for i in range(4):
+                    first = (h * 4 + i) * P
+                    nc.tensor.transpose(banks[s, h][:, i * P : (i + 1) * P], words[:, first : first + P], ident_f[:])
+
+        def item_out(s):
+            for h in range(2):
+                bank = banks[s, h]
+                if s < Z_ITEMS:
+                    nc.scalar.copy(
+                        out=z_grouped[s][:]
+                        .bitcast(F32)
+                        .rearrange("q (k pj lg h y) -> q k pj lg h y", k=NK, pj=2, h=2, y=4)[:, :, :, :, h, :],
+                        in_=bank[:].rearrange("q (y pj k lg) -> q k pj lg y", y=4, pj=2, k=NK),
+                    )
+                else:
+                    first = ((s - Z_ITEMS) * 2 + h) * 512
+                    nc.scalar.copy(
+                        out=w_grouped[:].bitcast(F32)[:, first : first + 512].rearrange("q (x r w) -> q x r w", x=2, w=2),
+                        in_=bank[:].rearrange("q (x w r) -> q x r w", x=2, w=2),
+                    )
+
+        def quantise_item(s):
+            if s < Z_ITEMS:
                 for k in range(NK):
                     nc.vector.quantize_mx(
                         out=z_codes[:, k * 512 + s * P : k * 512 + (s + 1) * P].bitcast(FP8X4),
                         scales=z_scales[:, k * 512 + s * P : k * 512 + (s + 1) * P],
-                        in_=z_grouped[:, k * 2048 + s * 512 : k * 2048 + (s + 1) * 512],
+                        in_=z_grouped[s][:, k * 512 : (k + 1) * 512],
                     )
             else:
-                j = s - 4
-                for h in range(j * 2, j * 2 + 2):
-                    nc.vector.tensor_scalar(
-                        out=w_grouped[:, h * 1024 : (h + 1) * 1024],
-                        in0=w_grouped[:, h * 1024 : (h + 1) * 1024],
-                        scalar1=w_gain[:, j : j + 1],
-                        scalar2=None,
-                        op0=ALU.mult,
-                    )
-                for h in range(j * 2, j * 2 + 2):
-                    nc.vector.quantize_mx(
-                        out=w_codes[:, h * 256 : (h + 1) * 256].bitcast(FP8X4),
-                        scales=w_scales[:, h * 256 : (h + 1) * 256],
-                        in_=w_grouped[:, h * 1024 : (h + 1) * 1024],
-                    )
-
-        x_codes = {}
-        x_scales = {}
-        t_rows = {}
-        t_codes = {}
-        t_scales = {}
-        o_sb = {}
-
-        def quantise_transposed(rows, codes, scales):
-            grouped = work.tile([P, 2048], BF16, align_bytes=64, tag="grouped", name="grouped", bufs=3)
-            grouped_words = grouped[:].bitcast(F32)
-            for half in range(2):
-                bank = psum.tile([P, 512], F32, tag="bank", name="bank_t")
-                for s in range(4):
-                    first = half * 512 + s * P
-                    nc.tensor.transpose(bank[:, s * P : (s + 1) * P], rows[:, first : first + P], ident_f[:])
-                nc.vector.tensor_copy(
-                    out=grouped_words[:, half * 512 : (half + 1) * 512].rearrange("q (c b w) -> q c b w", c=2, w=2),
-                    in_=bank[:].rearrange("q (c w b) -> q c b w", c=2, w=2),
-                )
-            for half in range(2):
+                j = s - Z_ITEMS
                 nc.vector.quantize_mx(
-                    out=codes[:, half * 256 : (half + 1) * 256].bitcast(FP8X4),
-                    scales=scales[:, half * 256 : (half + 1) * 256],
-                    in_=grouped[:, half * 1024 : (half + 1) * 1024],
+                    out=w_codes[:, j * 512 : (j + 1) * 512].bitcast(FP8X4),
+                    scales=w_scales[:, j * 512 : (j + 1) * 512],
+                    in_=w_grouped[:, j * 2048 : (j + 1) * 2048],
                 )
 
-        def quantise_x(n):
-            x_codes[n] = work.tile([P, NK * P], U32, align_bytes=64, tag="x_codes", name="x_codes", bufs=3)
-            x_scales[n] = work.tile([P, NK * P], U8, align_bytes=64, tag="x_scales", name="x_scales", bufs=3)
-            quantise_transposed(x_sb[n][:].bitcast(F32), x_codes[n], x_scales[n])
+        codes = {}
+        scales = {}
+        t_rows = {}
+        o_sb = {}
+        grouped = {}
+
+        def transpose_rows(key, rows):
+            for h in range(2):
+                banks[key, h] = psum.tile([P, 512], F32, tag="bank", name="bank_t")
+                for s in range(4):
+                    first = h * 512 + s * P
+                    nc.tensor.transpose(banks[key, h][:, s * P : (s + 1) * P], rows[:, first : first + P], ident_f[:])
+
+        def rows_out(key, h, copy):
+            if h == 0:
+                grouped[key] = work.tile([P, 2048], BF16, align_bytes=64, tag="grouped", name="grouped", bufs=5)
+            copy(
+                out=grouped[key][:].bitcast(F32)[:, h * 512 : (h + 1) * 512].rearrange("q (c b w) -> q c b w", c=2, w=2),
+                in_=banks[key, h][:].rearrange("q (c w b) -> q c b w", c=2, w=2),
+            )
+
+        def quantise_rows(key, h):
+            kind, n = key
+            if h == 0:
+                codes[key] = work.tile([P, 512], U32, align_bytes=64, tag="codes_" + kind, name="codes", bufs=8)
+                scales[key] = work.tile([P, 512], U8, align_bytes=64, tag="scales_" + kind, name="scales", bufs=8)
+            nc.vector.quantize_mx(
+                out=codes[key][:, h * 256 : (h + 1) * 256].bitcast(FP8X4),
+                scales=scales[key][:, h * 256 : (h + 1) * 256],
+                in_=grouped[key][:, h * 1024 : (h + 1) * 1024],
+            )
+
+        t_ps = {}
+        o_ps = {}
 
         def first_matmul(n, k):
-            if k == 0:
-                t_rows[n] = work.tile([P, 2048], BF16, tag="t_rows", name="t_rows", bufs=3)
-            t_ps = psum.tile([P, 512], F32, tag="bank")
+            t_ps[n, k] = psum.tile([P, 512], F32, tag="bank", name="t_ps")
             nc.tensor.matmul_mx(
-                out=t_ps[:],
-                lhsT=x_codes[n][:, k * P : (k + 1) * P].bitcast(FP8X4),
-                lhsT_scale=x_scales[n][:, k * P : (k + 1) * P],
+                out=t_ps[n, k][:],
+                lhsT=codes["x", n][:, k * P : (k + 1) * P].bitcast(FP8X4),
+                lhsT_scale=scales["x", n][:, k * P : (k + 1) * P],
                 rhs=z_codes[:, k * 512 : (k + 1) * 512].bitcast(FP8X4),
                 rhs_scale=z_scales[:, k * 512 : (k + 1) * 512],
                 start=True,
                 stop=True,
             )
-            nc.scalar.copy(
-                out=t_rows[n][:].rearrange("b (jv k p y) -> b jv k p y", jv=8, k=NK, p=NP)[:, :, k, :, :],
-                in_=t_ps[:].rearrange("b (p jv y) -> b jv p y", p=NP, jv=8),
+
+        def t_out(n, k, copy):
+            if k == 0:
+                t_rows[n] = work.tile([P, 2048], BF16, tag="t_rows", name="t_rows", bufs=3)
+            copy(
+                out=t_rows[n][:].rearrange("b (jw p k y) -> b jw p k y", jw=8, p=NP, k=NK)[:, :, :, k, :],
+                in_=t_ps[n, k][:].rearrange("b (p jw y) -> b jw p y", p=NP, jw=8),
             )
 
-        def quantise_t(n):
-            t_codes[n] = work.tile([P, NJ * P], U32, align_bytes=64, tag="t_codes", name="t_codes", bufs=4)
-            t_scales[n] = work.tile([P, NJ * P], U8, align_bytes=64, tag="t_scales", name="t_scales", bufs=4)
-            quantise_transposed(t_rows[n][:].bitcast(F32), t_codes[n], t_scales[n])
-
         def second_matmul(n, j):
-            if j == 0:
-                o_sb[n] = work.tile([P, NJ * M], F32, tag="o_sb", name="o_sb", bufs=3)
-            o_ps = psum.tile([P, 512], F32, tag="bank")
+            o_ps[n, j] = psum.tile([P, 512], F32, tag="bank", name="o_ps")
             nc.tensor.matmul_mx(
-                out=o_ps[:],
-                lhsT=t_codes[n][:, j * P : (j + 1) * P].bitcast(FP8X4),
-                lhsT_scale=t_scales[n][:, j * P : (j + 1) * P],
+                out=o_ps[n, j][:],
+                lhsT=codes["t", n][:, j * P : (j + 1) * P].bitcast(FP8X4),
+                lhsT_scale=scales["t", n][:, j * P : (j + 1) * P],
                 rhs=w_codes[:, j * 512 : (j + 1) * 512].bitcast(FP8X4),
                 rhs_scale=w_scales[:, j * 512 : (j + 1) * 512],
                 start=True,
                 stop=True,
             )
-            if j == NJ - 1:
-                nc.vector.tensor_copy(out=o_sb[n][:, j * M : (j + 1) * M], in_=o_ps[:])
-            else:
-                nc.scalar.copy(out=o_sb[n][:, j * M : (j + 1) * M], in_=o_ps[:])
+
+        def o_out(n, j, copy):
+            if j == 0:
+                o_sb[n] = work.tile([P, NJ * M], F32, tag="o_sb", name="o_sb", bufs=3)
+            copy(
+                out=o_sb[n][:, j * M : (j + 1) * M].rearrange("b (r mc) -> b r mc", mc=4),
+                in_=o_ps[n, j][:].rearrange("b (mc r) -> b r mc", mc=4),
+            )
             nc.sync.dma_start(out=out_rows[n * P : (n + 1) * P, j * M : (j + 1) * M], in_=o_sb[n][:, j * M : (j + 1) * M])
 
         def is_item(s):
-            return 0 <= s < PREP_ITEMS
+            return 0 <= s < ITEMS
+
+        def is_z(s):
+            return 0 <= s < Z_ITEMS
+
+        def is_y(s):
+            return Z_ITEMS <= s < ITEMS
 
         def is_tile(n):
             return 0 <= n < B_TILES
 
-        for step in range(PREP_ITEMS + B_TILES + 3):
+        scalar, vector = nc.scalar.copy, nc.vector.tensor_copy
+        for step in range(ITEMS + 2):
             if is_item(step):
-                magnitudes(step)
-            if is_item(step - 1):
-                column_sums_out(step - 1)
-            if is_item(step):
-                signs(step)
-                column_sums(step)
+                clamp_above(step)
             if is_item(step - 1):
                 sum_blocks(step - 1)
-            if is_item(step - 2):
-                scales_of(step - 2)
-                finish(step - 2)
-            n = step - PREP_ITEMS
-            for j in range(NJ):
-                if is_tile(n - 3):
+            if is_z(step - 3):
+                quantise_item(step - 3)
+            if is_item(step):
+                sums_raw(step)
+            if is_y(step - 2):
+                scale(step - 2)
+            if is_item(step):
+                sums_low(step)
+            if is_y(step - 2):
+                quantise_item(step - 2)
+            if is_item(step - 1):
+                gain_of(step - 1)
+            if is_tile(step):
+                transpose_rows(("x", step), x_sb[step][:].bitcast(F32))
+            if is_z(step - 1):
+                scale(step - 1)
+            if is_tile(step - 1):
+                for h in range(2):
+                    quantise_rows(("x", step - 1), h)
+            if is_item(step):
+                sums_out(step)
+            if is_y(step):
+                transpose_item(step)
+            if is_z(step - 1):
+                transpose_item(step - 1)
+            if is_tile(step):
+                for h in range(2):
+                    rows_out(("x", step), h, scalar)
+            if is_y(step):
+                item_out(step)
+            if is_z(step - 1):
+                item_out(step - 1)
+
+        for n in range(B_TILES + 3):
+            if is_tile(n):
+                for k in (0, 1):
+                    first_matmul(n, k)
+            if is_tile(n - 3):
+                for j in range(NJ):
                     second_matmul(n - 3, j)
-            if is_tile(n + 1):
-                quantise_x(n + 1)
-            for k in range(NK):
-                if is_tile(n):
+                for j in (0, 1):
+                    o_out(n - 3, j, vector if j % 2 else scalar)
+            if is_tile(n - 2):
+                quantise_rows(("t", n - 2), 0)
+            if is_tile(n - 3):
+                for j in (2, 3):
+                    o_out(n - 3, j, vector if j % 2 else scalar)
+            if is_tile(n - 2):
+                quantise_rows(("t", n - 2), 1)
+            if is_tile(n):
+                for k in (2, 3):
                     first_matmul(n, k)
             if is_tile(n - 1):
-                quantise_t(n - 1)
+                transpose_rows(("t", n - 1), t_rows[n - 1][:].bitcast(F32))
+                for h in range(2):
+                    rows_out(("t", n - 1), h, vector)
+            if is_tile(n):
+                for k in range(NK):
+                    t_out(n, k, scalar)

@@ -19,6 +19,7 @@ B_TILES = B // P
 BLOCK_ELEMS = M * L
 TINY = 2.0**-100
 Z_ITEMS = 4
+SUM_COLS = 48
 ITEMS = Z_ITEMS + NJ
 FLOPS = 2 * (2 * B * N * NP * NJ * NK * L)
 
@@ -59,12 +60,9 @@ def tile_bqqlinear_pa_kernel(tc, x_q, Y_fp, Z_fp, a_core, out):
         make_identity(nc, ident_f[:])
         ones_f = const.tile([P, P], F32)
         nc.vector.memset(ones_f[:], 1.0)
-        pick_g = const.tile([P, 64], BF16)
+        pick_g = const.tile([P, 8 * SUM_COLS], BF16)
         nc.vector.memset(pick_g[:], 0.0)
-        nc.vector.memset(pick_g[:, 0:64:9], 1.0)
-        pick_h = const.tile([P, 4], BF16)
-        nc.vector.memset(pick_h[:], 0.0)
-        nc.vector.memset(pick_h[:, 0:4:3], 1.0)
+        nc.vector.memset(pick_g[:, 0 : 8 * SUM_COLS : SUM_COLS + 1], 1.0)
         same_g4 = const.tile([P, P], F32)
         nc.vector.memset(same_g4[:], 0.0)
         for i in range(4):
@@ -86,10 +84,12 @@ def tile_bqqlinear_pa_kernel(tc, x_q, Y_fp, Z_fp, a_core, out):
             in1=own[:, 0:8].rearrange("q (p k) -> q p k", p=NP).unsqueeze(1).to_broadcast([P, NJ, NP, NK]),
             op=ALU.mult,
         )
-        pick_z = const.tile([P, 8], BF16)
-        nc.vector.tensor_copy(out=pick_z[:], in_=own[:, 0:8])
-        pick_z2 = const.tile([P, 8], BF16)
-        nc.vector.tensor_scalar(out=pick_z2[:], in0=own[:, 0:8], scalar1=-2.0, scalar2=None, op0=ALU.mult)
+        pick_z = const.tile([P, SUM_COLS], BF16)
+        nc.vector.memset(pick_z[:], 0.0)
+        nc.vector.tensor_copy(out=pick_z[:, 0:8], in_=own[:, 0:8])
+        pick_z2 = const.tile([P, SUM_COLS], BF16)
+        nc.vector.memset(pick_z2[:], 0.0)
+        nc.vector.tensor_scalar(out=pick_z2[:, 0:8], in0=own[:, 0:8], scalar1=-2.0, scalar2=None, op0=ALU.mult)
         nc.vector.tensor_scalar(out=own[:, 8:10], in0=halves[:], scalar1=-2.0, scalar2=None, op0=ALU.mult)
         a_sum = const.tile([P, NJ], F32)
         nc.vector.tensor_reduce(
@@ -127,14 +127,14 @@ def tile_bqqlinear_pa_kernel(tc, x_q, Y_fp, Z_fp, a_core, out):
             for c in range(16):
                 if s < Z_ITEMS:
                     nc.tensor.matmul(
-                        out=col_sums[s][:, 0:8], lhsT=raw[s][:, c * P : (c + 1) * P], rhs=pick_z[:], start=(c == 0), stop=False
+                        out=col_sums[s][:, 0:SUM_COLS], lhsT=raw[s][:, c * P : (c + 1) * P], rhs=pick_z[:], start=(c == 0), stop=False
                     )
                 else:
                     g = c // 2
                     nc.tensor.matmul(
-                        out=col_sums[s][:, 0:8],
+                        out=col_sums[s][:, 0:SUM_COLS],
                         lhsT=raw[s][:, c * P : (c + 1) * P],
-                        rhs=pick_g[:, g * 8 : (g + 1) * 8],
+                        rhs=pick_g[:, g * SUM_COLS : (g + 1) * SUM_COLS],
                         start=(c == 0),
                         stop=(c == 15),
                     )
@@ -143,14 +143,14 @@ def tile_bqqlinear_pa_kernel(tc, x_q, Y_fp, Z_fp, a_core, out):
             for c in range(16):
                 if s < Z_ITEMS:
                     nc.tensor.matmul(
-                        out=col_sums[s][:, 0:8], lhsT=low[s][:, c * P : (c + 1) * P], rhs=pick_z2[:], start=False, stop=(c == 15)
+                        out=col_sums[s][:, 0:SUM_COLS], lhsT=low[s][:, c * P : (c + 1) * P], rhs=pick_z2[:], start=False, stop=(c == 15)
                     )
                 else:
                     h = c % 2
                     nc.tensor.matmul(
-                        out=col_sums[s][:, 8:10],
+                        out=col_sums[s][:, 8 : 8 + SUM_COLS],
                         lhsT=low[s][:, c * P : (c + 1) * P],
-                        rhs=pick_h[:, h * 2 : (h + 1) * 2],
+                        rhs=pick_g[:, h * SUM_COLS : (h + 1) * SUM_COLS],
                         start=(c == 0),
                         stop=(c == 15),
                     )

@@ -37,7 +37,6 @@ def tile_bqqlinear_pa_kernel(tc, x_q, Y_fp, Z_fp, a_core, out):
         ctx.enter_context(tc.manual_schedule())
 
         a_all = const.tile([P, NP * NJ * NK], BF16)
-        nc.scalar.dma_start(out=a_all[:], in_=a_core.rearrange("p j k -> (p j k)").partition_broadcast(P))
         raw = [const.tile([P, 2048], BF16, name="raw%d" % s) for s in range(ITEMS)]
         x_sb = [const.tile([P, NK * N], BF16, name="x_sb%d" % n) for n in range(B_TILES)]
 
@@ -55,6 +54,8 @@ def tile_bqqlinear_pa_kernel(tc, x_q, Y_fp, Z_fp, a_core, out):
         for s in range(ITEMS):
             load_item(s)
             nc.sync.dma_start(out=x_sb[s][:], in_=x_rows[s * P : (s + 1) * P, :])
+            if s == 1:
+                nc.sync.dma_start(out=a_all[:], in_=a_core.rearrange("p j k -> (p j k)").partition_broadcast(P))
 
         ident_f = const.tile([P, P], F32)
         make_identity(nc, ident_f[:])
@@ -77,13 +78,6 @@ def tile_bqqlinear_pa_kernel(tc, x_q, Y_fp, Z_fp, a_core, out):
         nc.vector.tensor_reduce(
             out=halves[:], in_=ident_f[:].rearrange("q (h x) -> q h x", h=2), axis=AX.X, op=ALU.add
         )
-        a_pick = const.tile([P, 32], F32)
-        nc.vector.tensor_tensor(
-            out=a_pick[:].rearrange("q (j p k) -> q j p k", j=NJ, p=NP),
-            in0=a_all[:].rearrange("q (p j k) -> q j p k", p=NP, j=NJ),
-            in1=own[:, 0:8].rearrange("q (p k) -> q p k", p=NP).unsqueeze(1).to_broadcast([P, NJ, NP, NK]),
-            op=ALU.mult,
-        )
         pick_z = const.tile([P, SUM_COLS], BF16)
         nc.vector.memset(pick_z[:], 0.0)
         nc.vector.tensor_copy(out=pick_z[:, 0:8], in_=own[:, 0:8])
@@ -91,14 +85,23 @@ def tile_bqqlinear_pa_kernel(tc, x_q, Y_fp, Z_fp, a_core, out):
         nc.vector.memset(pick_z2[:], 0.0)
         nc.vector.tensor_scalar(out=pick_z2[:, 0:8], in0=own[:, 0:8], scalar1=-2.0, scalar2=None, op0=ALU.mult)
         nc.vector.tensor_scalar(out=own[:, 8:10], in0=halves[:], scalar1=-2.0, scalar2=None, op0=ALU.mult)
+        a_pick = const.tile([P, 32], F32)
         a_sum = const.tile([P, NJ], F32)
-        nc.vector.tensor_reduce(
-            out=a_sum[:], in_=a_pick[:].rearrange("q (j g) -> q j g", j=NJ), axis=AX.X, op=ALU.add
-        )
         a_own = const.tile([P, NJ], F32)
-        nc.vector.tensor_scalar(
-            out=a_own[:], in0=a_sum[:], scalar1=1.0 / (TINY * BLOCK_ELEMS), scalar2=None, op0=ALU.mult
-        )
+
+        def own_a():
+            nc.vector.tensor_tensor(
+                out=a_pick[:].rearrange("q (j p k) -> q j p k", j=NJ, p=NP),
+                in0=a_all[:].rearrange("q (p j k) -> q j p k", p=NP, j=NJ),
+                in1=own[:, 0:8].rearrange("q (p k) -> q p k", p=NP).unsqueeze(1).to_broadcast([P, NJ, NP, NK]),
+                op=ALU.mult,
+            )
+            nc.vector.tensor_reduce(
+                out=a_sum[:], in_=a_pick[:].rearrange("q (j g) -> q j g", j=NJ), axis=AX.X, op=ALU.add
+            )
+            nc.vector.tensor_scalar(
+                out=a_own[:], in0=a_sum[:], scalar1=1.0 / (TINY * BLOCK_ELEMS), scalar2=None, op0=ALU.mult
+            )
 
         z_grouped = [const.tile([P, 2048], BF16, align_bytes=64, name="z_grouped%d" % s) for s in range(Z_ITEMS)]
         z_codes = const.tile([P, NK * 512], U32, align_bytes=64)
@@ -320,29 +323,32 @@ def tile_bqqlinear_pa_kernel(tc, x_q, Y_fp, Z_fp, a_core, out):
 
         scalar, vector = nc.scalar.copy, nc.vector.tensor_copy
         for step in range(ITEMS + 2):
+            if step == 3:
+                own_a()
             if is_item(step):
                 clamp_above(step)
+            if is_y(step - 2):
+                scale(step - 2)
             if is_item(step - 1):
                 sum_blocks(step - 1)
             if is_z(step - 3):
                 quantise_item(step - 3)
             if is_item(step):
                 sums_raw(step)
-            if is_y(step - 2):
-                scale(step - 2)
             if is_item(step):
                 sums_low(step)
-            if is_y(step - 2):
-                quantise_item(step - 2)
             if is_item(step - 1):
                 gain_of(step - 1)
+            if is_y(step - 2):
+                quantise_item(step - 2)
             if is_tile(step):
                 transpose_rows(("x", step), x_sb[step][:].bitcast(F32))
+            if is_tile(step - 1):
+                quantise_rows(("x", step - 1), 0)
             if is_z(step - 1):
                 scale(step - 1)
             if is_tile(step - 1):
-                for h in range(2):
-                    quantise_rows(("x", step - 1), h)
+                quantise_rows(("x", step - 1), 1)
             if is_item(step):
                 sums_out(step)
             if is_y(step):
@@ -351,7 +357,7 @@ def tile_bqqlinear_pa_kernel(tc, x_q, Y_fp, Z_fp, a_core, out):
                 transpose_item(step - 1)
             if is_tile(step):
                 for h in range(2):
-                    rows_out(("x", step), h, scalar)
+                    rows_out(("x", step), h, vector if step >= 7 else scalar)
             if is_y(step):
                 item_out(step)
             if is_z(step - 1):
@@ -365,12 +371,12 @@ def tile_bqqlinear_pa_kernel(tc, x_q, Y_fp, Z_fp, a_core, out):
                 for j in range(NJ):
                     second_matmul(n - 3, j)
                 for j in (0, 1):
-                    o_out(n - 3, j, vector if j % 2 else scalar)
+                    o_out(n - 3, j, vector if j % 2 and n - 3 != B_TILES - 2 else scalar)
             if is_tile(n - 2):
                 quantise_rows(("t", n - 2), 0)
             if is_tile(n - 3):
                 for j in (2, 3):
-                    o_out(n - 3, j, vector if j % 2 else scalar)
+                    o_out(n - 3, j, vector if j % 2 and n - 3 != B_TILES - 2 else scalar)
             if is_tile(n - 2):
                 quantise_rows(("t", n - 2), 1)
             if is_tile(n):

@@ -112,7 +112,9 @@ def tile_bqqlinear_pa_kernel(tc, x_q, Y_fp, Z_fp, a_core, out):
         gain = const.tile([P, ITEMS], F32)
         low = {}
         col_sums = {}
-        col_sums_sb = {}
+        col_sums_sb = [const.tile([P, 64], F32, name="col_sums_sb%d" % i) for i in range(2)]
+        for i in range(2):
+            nc.vector.memset(col_sums_sb[i][:], 0.0)
         block_sums = {}
         banks = {}
 
@@ -125,9 +127,10 @@ def tile_bqqlinear_pa_kernel(tc, x_q, Y_fp, Z_fp, a_core, out):
                 i = raw[s][:].rearrange("r (g mw y) -> r mw g y", mw=8, g=8)
             nc.vector.tensor_scalar(out=o, in0=i, scalar1=TINY, scalar2=None, op0=ALU.min)
 
-        def sums_raw(s):
-            col_sums[s] = psum.tile([P, 512], F32, tag="bank", name="col_sums")
-            for c in range(16):
+        def sums_raw(s, h):
+            if h == 0:
+                col_sums[s] = psum.tile([P, 512], F32, tag="bank", name="col_sums")
+            for c in range(8 * h, 8 * h + 8):
                 if s < Z_ITEMS:
                     nc.tensor.matmul(
                         out=col_sums[s][:, 0:SUM_COLS], lhsT=raw[s][:, c * P : (c + 1) * P], rhs=pick_z[:], start=(c == 0), stop=False
@@ -142,35 +145,34 @@ def tile_bqqlinear_pa_kernel(tc, x_q, Y_fp, Z_fp, a_core, out):
                         stop=(c == 15),
                     )
 
-        def sums_low(s):
-            for c in range(16):
+        def sums_low(s, h):
+            for c in range(8 * h, 8 * h + 8):
                 if s < Z_ITEMS:
                     nc.tensor.matmul(
                         out=col_sums[s][:, 0:SUM_COLS], lhsT=low[s][:, c * P : (c + 1) * P], rhs=pick_z2[:], start=False, stop=(c == 15)
                     )
                 else:
-                    h = c % 2
+                    gh = c % 2
                     nc.tensor.matmul(
                         out=col_sums[s][:, 8 : 8 + SUM_COLS],
                         lhsT=low[s][:, c * P : (c + 1) * P],
-                        rhs=pick_g[:, h * SUM_COLS : (h + 1) * SUM_COLS],
+                        rhs=pick_g[:, gh * SUM_COLS : (gh + 1) * SUM_COLS],
                         start=(c == 0),
                         stop=(c == 15),
                     )
 
         def sums_out(s):
-            col_sums_sb[s] = work.tile([P, 10], F32, tag="col_sums_sb", name="col_sums_sb")
             width = 8 if s < Z_ITEMS else 10
-            nc.scalar.copy(out=col_sums_sb[s][:, 0:width], in_=col_sums[s][:, 0:width])
+            nc.scalar.copy(out=col_sums_sb[s % 2][:, 0:width], in_=col_sums[s][:, 0:width])
 
         def sum_blocks(s):
             block_sums[s] = psum.tile([P, 512], F32, tag="bank", name="block_sums")
             nc.tensor.matmul(
-                out=block_sums[s][:, 0:8], lhsT=ones_f[:], rhs=col_sums_sb[s][:, 0:8], start=True, stop=True
+                out=block_sums[s][:, 0:64], lhsT=ones_f[:], rhs=col_sums_sb[s % 2][:], start=True, stop=True
             )
             if s >= Z_ITEMS:
                 nc.tensor.matmul(
-                    out=block_sums[s][:, 8:10], lhsT=same_g4[:], rhs=col_sums_sb[s][:, 8:10], start=True, stop=True
+                    out=block_sums[s][:, 8:64], lhsT=same_g4[:], rhs=col_sums_sb[s % 2][:, 8:64], start=True, stop=True
                 )
 
         def gain_of(s):
@@ -192,13 +194,12 @@ def tile_bqqlinear_pa_kernel(tc, x_q, Y_fp, Z_fp, a_core, out):
                 out=part, in0=part, scalar1=-TINY, scalar2=gain[:, s : s + 1], op0=ALU.max, op1=ALU.mult
             )
 
-        def transpose_item(s):
+        def transpose_item(s, h):
             words = low[s][:].bitcast(F32)
-            for h in range(2):
-                banks[s, h] = psum.tile([P, 512], F32, tag="bank", name="bank_w")
-                for i in range(4):
-                    first = (h * 4 + i) * P
-                    nc.tensor.transpose(banks[s, h][:, i * P : (i + 1) * P], words[:, first : first + P], ident_f[:])
+            banks[s, h] = psum.tile([P, 512], F32, tag="bank", name="bank_w")
+            for i in range(4):
+                first = (h * 4 + i) * P
+                nc.tensor.transpose(banks[s, h][:, i * P : (i + 1) * P], words[:, first : first + P], ident_f[:])
 
         def item_out(s):
             for h in range(2):
@@ -239,12 +240,11 @@ def tile_bqqlinear_pa_kernel(tc, x_q, Y_fp, Z_fp, a_core, out):
         o_sb = {}
         grouped = {}
 
-        def transpose_rows(key, rows):
-            for h in range(2):
-                banks[key, h] = psum.tile([P, 512], F32, tag="bank", name="bank_t")
-                for s in range(4):
-                    first = h * 512 + s * P
-                    nc.tensor.transpose(banks[key, h][:, s * P : (s + 1) * P], rows[:, first : first + P], ident_f[:])
+        def transpose_rows(key, rows, h):
+            banks[key, h] = psum.tile([P, 512], F32, tag="bank", name="bank_t")
+            for s in range(4):
+                first = h * 512 + s * P
+                nc.tensor.transpose(banks[key, h][:, s * P : (s + 1) * P], rows[:, first : first + P], ident_f[:])
 
         def rows_out(key, h, copy):
             if h == 0:
@@ -334,15 +334,21 @@ def tile_bqqlinear_pa_kernel(tc, x_q, Y_fp, Z_fp, a_core, out):
             if is_z(step - 3):
                 quantise_item(step - 3)
             if is_item(step):
-                sums_raw(step)
+                sums_raw(step, 0)
             if is_item(step):
-                sums_low(step)
+                sums_raw(step, 1)
+            if is_item(step):
+                sums_low(step, 0)
+            if is_item(step):
+                sums_low(step, 1)
             if is_item(step - 1):
                 gain_of(step - 1)
             if is_y(step - 2):
                 quantise_item(step - 2)
             if is_tile(step):
-                transpose_rows(("x", step), x_sb[step][:].bitcast(F32))
+                transpose_rows(("x", step), x_sb[step][:].bitcast(F32), 0)
+            if is_tile(step):
+                transpose_rows(("x", step), x_sb[step][:].bitcast(F32), 1)
             if is_tile(step - 1):
                 quantise_rows(("x", step - 1), 0)
             if is_z(step - 1):
@@ -352,12 +358,17 @@ def tile_bqqlinear_pa_kernel(tc, x_q, Y_fp, Z_fp, a_core, out):
             if is_item(step):
                 sums_out(step)
             if is_y(step):
-                transpose_item(step)
+                transpose_item(step, 0)
+            if is_y(step):
+                transpose_item(step, 1)
             if is_z(step - 1):
-                transpose_item(step - 1)
+                transpose_item(step - 1, 0)
+            if is_z(step - 1):
+                transpose_item(step - 1, 1)
             if is_tile(step):
-                for h in range(2):
-                    rows_out(("x", step), h, vector if step >= 7 else scalar)
+                rows_out(("x", step), 0, vector if step >= 7 else scalar)
+            if is_tile(step):
+                rows_out(("x", step), 1, vector if step >= 7 else scalar)
             if is_y(step):
                 item_out(step)
             if is_z(step - 1):
@@ -383,7 +394,8 @@ def tile_bqqlinear_pa_kernel(tc, x_q, Y_fp, Z_fp, a_core, out):
                 for k in (2, 3):
                     first_matmul(n, k)
             if is_tile(n - 1):
-                transpose_rows(("t", n - 1), t_rows[n - 1][:].bitcast(F32))
+                for h in range(2):
+                    transpose_rows(("t", n - 1), t_rows[n - 1][:].bitcast(F32), h)
                 for h in range(2):
                     rows_out(("t", n - 1), h, vector)
             if is_tile(n):

@@ -51,8 +51,10 @@ def tile_bqqlinear_pa_kernel(tc, x_q, Y_fp, Z_fp, a_core, out):
                             in_=Y_fp[p, s - Z_ITEMS].rearrange("k (r mc) l -> r k (mc l)", mc=4),
                         )
 
+        load_item(0)
         for s in range(ITEMS):
-            load_item(s)
+            if s + 1 < ITEMS:
+                load_item(s + 1)
             nc.sync.dma_start(out=x_sb[s][:], in_=x_rows[s * P : (s + 1) * P, :])
             if s == 1:
                 nc.sync.dma_start(out=a_all[:], in_=a_core.rearrange("p j k -> (p j k)").partition_broadcast(P))
@@ -322,7 +324,7 @@ def tile_bqqlinear_pa_kernel(tc, x_q, Y_fp, Z_fp, a_core, out):
             return 0 <= n < B_TILES
 
         scalar, vector = nc.scalar.copy, nc.vector.tensor_copy
-        for step in range(ITEMS + 2):
+        for step in range(ITEMS + 3):
             if step == 3:
                 own_a()
             if is_item(step):
@@ -345,16 +347,16 @@ def tile_bqqlinear_pa_kernel(tc, x_q, Y_fp, Z_fp, a_core, out):
                 gain_of(step - 1)
             if is_y(step - 2):
                 quantise_item(step - 2)
-            if is_tile(step):
-                transpose_rows(("x", step), x_sb[step][:].bitcast(F32), 0)
-            if is_tile(step):
-                transpose_rows(("x", step), x_sb[step][:].bitcast(F32), 1)
             if is_tile(step - 1):
-                quantise_rows(("x", step - 1), 0)
+                transpose_rows(("x", step - 1), x_sb[step - 1][:].bitcast(F32), 0)
+            if is_tile(step - 1):
+                transpose_rows(("x", step - 1), x_sb[step - 1][:].bitcast(F32), 1)
+            if is_tile(step - 2):
+                quantise_rows(("x", step - 2), 0)
             if is_z(step - 1):
                 scale(step - 1)
-            if is_tile(step - 1):
-                quantise_rows(("x", step - 1), 1)
+            if is_tile(step - 2):
+                quantise_rows(("x", step - 2), 1)
             if is_item(step):
                 sums_out(step)
             if is_y(step):
@@ -365,10 +367,10 @@ def tile_bqqlinear_pa_kernel(tc, x_q, Y_fp, Z_fp, a_core, out):
                 transpose_item(step - 1, 0)
             if is_z(step - 1):
                 transpose_item(step - 1, 1)
-            if is_tile(step):
-                rows_out(("x", step), 0, vector if step >= 7 else scalar)
-            if is_tile(step):
-                rows_out(("x", step), 1, vector if step >= 7 else scalar)
+            if is_tile(step - 1):
+                rows_out(("x", step - 1), 0, vector if step >= 8 else scalar)
+            if is_tile(step - 1):
+                rows_out(("x", step - 1), 1, vector if step >= 8 else scalar)
             if is_y(step):
                 item_out(step)
             if is_z(step - 1):

@@ -333,8 +333,6 @@ def tile_bqqlinear_pa_kernel(tc, x_q, Y_fp, Z_fp, a_core, out):
                 scale(step - 2)
             if is_item(step - 1):
                 sum_blocks(step - 1)
-            if is_z(step - 3):
-                quantise_item(step - 3)
             if is_item(step):
                 sums_raw(step, 0)
             if is_item(step):
@@ -345,8 +343,6 @@ def tile_bqqlinear_pa_kernel(tc, x_q, Y_fp, Z_fp, a_core, out):
                 sums_low(step, 1)
             if is_item(step - 1):
                 gain_of(step - 1)
-            if is_y(step - 2):
-                quantise_item(step - 2)
             if is_tile(step - 1):
                 transpose_rows(("x", step - 1), x_sb[step - 1][:].bitcast(F32), 0)
             if is_tile(step - 1):
@@ -355,8 +351,12 @@ def tile_bqqlinear_pa_kernel(tc, x_q, Y_fp, Z_fp, a_core, out):
                 quantise_rows(("x", step - 2), 0)
             if is_z(step - 1):
                 scale(step - 1)
+            if is_z(step - 3):
+                quantise_item(step - 3)
             if is_tile(step - 2):
                 quantise_rows(("x", step - 2), 1)
+            if is_y(step - 2):
+                quantise_item(step - 2)
             if is_item(step):
                 sums_out(step)
             if is_y(step):
@@ -381,8 +381,12 @@ def tile_bqqlinear_pa_kernel(tc, x_q, Y_fp, Z_fp, a_core, out):
                 for k in (0, 1):
                     first_matmul(n, k)
             if is_tile(n - 3):
-                for j in range(NJ):
+                for j in (0, 1):
                     second_matmul(n - 3, j)
+            if is_tile(n - 3):
+                for j in (2, 3):
+                    second_matmul(n - 3, j)
+            if is_tile(n - 3):
                 for j in (0, 1):
                     o_out(n - 3, j, vector if j % 2 and n - 3 != B_TILES - 2 else scalar)
             if is_tile(n - 2):
@@ -396,10 +400,16 @@ def tile_bqqlinear_pa_kernel(tc, x_q, Y_fp, Z_fp, a_core, out):
                 for k in (2, 3):
                     first_matmul(n, k)
             if is_tile(n - 1):
-                for h in range(2):
-                    transpose_rows(("t", n - 1), t_rows[n - 1][:].bitcast(F32), h)
-                for h in range(2):
-                    rows_out(("t", n - 1), h, vector)
+                transpose_rows(("t", n - 1), t_rows[n - 1][:].bitcast(F32), 0)
+            if is_tile(n - 1):
+                transpose_rows(("t", n - 1), t_rows[n - 1][:].bitcast(F32), 1)
+            if is_tile(n - 1):
+                rows_out(("t", n - 1), 0, vector)
+            if is_tile(n - 1):
+                rows_out(("t", n - 1), 1, vector)
             if is_tile(n):
-                for k in range(NK):
+                for k in (0, 1):
+                    t_out(n, k, scalar)
+            if is_tile(n):
+                for k in (2, 3):
                     t_out(n, k, scalar)

@@ -388,12 +388,12 @@ def tile_bqqlinear_pa_kernel(tc, x_q, Y_fp, Z_fp, a_core, out):
                     second_matmul(n - 3, j)
             if is_tile(n - 3):
                 for j in (0, 1):
-                    o_out(n - 3, j, vector if j % 2 and n - 3 != B_TILES - 2 else scalar)
+                    o_out(n - 3, j, vector if (j % 2 or (j == 2 and (n - 3) % 3 == 0)) and n - 3 != B_TILES - 2 else scalar)
             if is_tile(n - 2):
                 quantise_rows(("t", n - 2), 0)
             if is_tile(n - 3):
                 for j in (2, 3):
-                    o_out(n - 3, j, vector if j % 2 and n - 3 != B_TILES - 2 else scalar)
+                    o_out(n - 3, j, vector if (j % 2 or (j == 2 and (n - 3) % 3 == 0)) and n - 3 != B_TILES - 2 else scalar)
             if is_tile(n - 2):
                 quantise_rows(("t", n - 2), 1)
             if is_tile(n):

@@ -106,11 +106,11 @@ def tile_bqqlinear_pa_kernel(tc, x_q, Y_fp, Z_fp, a_core, out):
             )
 
         z_grouped = [const.tile([P, 2048], BF16, align_bytes=64, name="z_grouped%d" % s) for s in range(Z_ITEMS)]
-        z_codes = const.tile([P, NK * 512], U32, align_bytes=64)
-        z_scales = const.tile([P, NK * 512], U8, align_bytes=64)
+        z_codes = const.tile([P, NK * 512], U32, align_bytes=256)
+        z_scales = const.tile([P, NK * 512], U8, align_bytes=256)
         w_grouped = const.tile([P, NJ * 2048], BF16, align_bytes=64)
-        w_codes = const.tile([P, NJ * 512], U32, align_bytes=64)
-        w_scales = const.tile([P, NJ * 512], U8, align_bytes=64)
+        w_codes = const.tile([P, NJ * 512], U32, align_bytes=256)
+        w_scales = const.tile([P, NJ * 512], U8, align_bytes=256)
         gain = const.tile([P, ITEMS], F32)
         low = {}
         col_sums = {}
@@ -259,8 +259,8 @@ def tile_bqqlinear_pa_kernel(tc, x_q, Y_fp, Z_fp, a_core, out):
         def quantise_rows(key, h):
             kind, n = key
             if h == 0:
-                codes[key] = work.tile([P, 512], U32, align_bytes=64, tag="codes_" + kind, name="codes", bufs=8)
-                scales[key] = work.tile([P, 512], U8, align_bytes=64, tag="scales_" + kind, name="scales", bufs=8)
+                codes[key] = work.tile([P, 512], U32, align_bytes=256, tag="codes_" + kind, name="codes", bufs=8)
+                scales[key] = work.tile([P, 512], U8, align_bytes=256, tag="scales_" + kind, name="scales", bufs=8)
             nc.vector.quantize_mx(
                 out=codes[key][:, h * 256 : (h + 1) * 256].bitcast(FP8X4),
                 scales=scales[key][:, h * 256 : (h + 1) * 256],

@@ -13,14 +13,17 @@ AX = mybir.AxisListType
 
 P = 128
 NP, NJ, NK = 2, 4, 4
+PAIRS = NP * NK
 M, L, N = 512, 64, 512
 B = 1024
 B_TILES = B // P
+BANK = 512
 BLOCK_ELEMS = M * L
 TINY = 2.0**-100
 Z_ITEMS = 4
-SUM_COLS = 48
 ITEMS = Z_ITEMS + NJ
+SUM_COLS = 48
+TOTAL_COLS = 64
 FLOPS = 2 * (2 * B * N * NP * NJ * NK * L)
 
 
@@ -37,35 +40,35 @@ def tile_bqqlinear_pa_kernel(tc, x_q, Y_fp, Z_fp, a_core, out):
         ctx.enter_context(tc.manual_schedule())
 
         a_all = const.tile([P, NP * NJ * NK], BF16)
-        raw = [const.tile([P, 2048], BF16, name="raw%d" % s) for s in range(ITEMS)]
+        weights = [const.tile([P, 2048], BF16, name="weights%d" % s) for s in range(ITEMS)]
         x_sb = [const.tile([P, NK * N], BF16, name="x_sb%d" % n) for n in range(B_TILES)]
 
         def load_item(s):
             if s < Z_ITEMS:
-                nc.sync.dma_start(out=raw[s][:], in_=z_chunks[s])
+                nc.sync.dma_start(out=weights[s][:], in_=z_chunks[s])
             else:
                 with nc.allow_non_contiguous_dma(reason="rows of four m, 256 bfloat16 values"):
                     for p in range(NP):
                         nc.sync.dma_start(
-                            out=raw[s][:, p * 1024 : (p + 1) * 1024].rearrange("r (k x) -> r k x", k=NK),
+                            out=weights[s][:, p * 1024 : (p + 1) * 1024].rearrange("r (k x) -> r k x", k=NK),
                             in_=Y_fp[p, s - Z_ITEMS].rearrange("k (r mc) l -> r k (mc l)", mc=4),
                         )
 
         load_item(0)
-        for s in range(ITEMS):
-            if s + 1 < ITEMS:
-                load_item(s + 1)
-            nc.sync.dma_start(out=x_sb[s][:], in_=x_rows[s * P : (s + 1) * P, :])
-            if s == 1:
+        for i in range(ITEMS):
+            if i + 1 < ITEMS:
+                load_item(i + 1)
+            nc.sync.dma_start(out=x_sb[i][:], in_=x_rows[i * P : (i + 1) * P, :])
+            if i == 1:
                 nc.sync.dma_start(out=a_all[:], in_=a_core.rearrange("p j k -> (p j k)").partition_broadcast(P))
 
         ident_f = const.tile([P, P], F32)
         make_identity(nc, ident_f[:])
         ones_f = const.tile([P, P], F32)
         nc.vector.memset(ones_f[:], 1.0)
-        pick_g = const.tile([P, 8 * SUM_COLS], BF16)
+        pick_g = const.tile([P, PAIRS * SUM_COLS], BF16)
         nc.vector.memset(pick_g[:], 0.0)
-        nc.vector.memset(pick_g[:, 0 : 8 * SUM_COLS : SUM_COLS + 1], 1.0)
+        nc.vector.memset(pick_g[:, 0 : PAIRS * SUM_COLS : SUM_COLS + 1], 1.0)
         same_g4 = const.tile([P, P], F32)
         nc.vector.memset(same_g4[:], 0.0)
         for i in range(4):
@@ -74,7 +77,7 @@ def tile_bqqlinear_pa_kernel(tc, x_q, Y_fp, Z_fp, a_core, out):
             )
         own = const.tile([P, 10], F32)
         nc.vector.tensor_reduce(
-            out=own[:, 0:8], in_=ident_f[:].rearrange("q (g lam) -> q g lam", g=8), axis=AX.X, op=ALU.add
+            out=own[:, 0:8], in_=ident_f[:].rearrange("q (g lam) -> q g lam", g=PAIRS), axis=AX.X, op=ALU.add
         )
         halves = const.tile([P, 2], F32)
         nc.vector.tensor_reduce(
@@ -87,7 +90,7 @@ def tile_bqqlinear_pa_kernel(tc, x_q, Y_fp, Z_fp, a_core, out):
         nc.vector.memset(pick_z2[:], 0.0)
         nc.vector.tensor_scalar(out=pick_z2[:, 0:8], in0=own[:, 0:8], scalar1=-2.0, scalar2=None, op0=ALU.mult)
         nc.vector.tensor_scalar(out=own[:, 8:10], in0=halves[:], scalar1=-2.0, scalar2=None, op0=ALU.mult)
-        a_pick = const.tile([P, 32], F32)
+        a_pick = const.tile([P, NJ * PAIRS], F32)
         a_sum = const.tile([P, NJ], F32)
         a_own = const.tile([P, NJ], F32)
 
@@ -111,73 +114,75 @@ def tile_bqqlinear_pa_kernel(tc, x_q, Y_fp, Z_fp, a_core, out):
         w_grouped = const.tile([P, NJ * 2048], BF16, align_bytes=64)
         w_codes = const.tile([P, NJ * 512], U32, align_bytes=256)
         w_scales = const.tile([P, NJ * 512], U8, align_bytes=256)
-        gain = const.tile([P, ITEMS], F32)
+        factor = const.tile([P, ITEMS], F32)
         low = {}
         col_sums = {}
-        col_sums_sb = [const.tile([P, 64], F32, name="col_sums_sb%d" % i) for i in range(2)]
+        col_sums_sb = [const.tile([P, TOTAL_COLS], F32, name="col_sums_sb%d" % i) for i in range(2)]
         for i in range(2):
             nc.vector.memset(col_sums_sb[i][:], 0.0)
         block_sums = {}
         banks = {}
 
         def clamp_above(s):
-            low[s] = work.tile([P, 2048], BF16, tag="low", name="low", bufs=4)
+            low[s] = work.tile([P, 2048], BF16, tag="low", name="low", bufs=5)
             if s < Z_ITEMS:
-                o, i = low[s][:], raw[s][:]
+                clamped, values = low[s][:], weights[s][:]
             else:
-                o = low[s][:].rearrange("r (mw g y) -> r mw g y", mw=8, g=8)
-                i = raw[s][:].rearrange("r (g mw y) -> r mw g y", mw=8, g=8)
-            nc.vector.tensor_scalar(out=o, in0=i, scalar1=TINY, scalar2=None, op0=ALU.min)
+                clamped = low[s][:].rearrange("r (mw g y) -> r mw g y", mw=8, g=PAIRS)
+                values = weights[s][:].rearrange("r (g mw y) -> r mw g y", mw=8, g=PAIRS)
+            nc.vector.tensor_scalar(out=clamped, in0=values, scalar1=TINY, scalar2=None, op0=ALU.min)
 
-        def sums_raw(s, h):
-            if h == 0:
-                col_sums[s] = psum.tile([P, 512], F32, tag="bank", name="col_sums")
-            for c in range(8 * h, 8 * h + 8):
+        def column_sums(s):
+            col_sums[s] = psum.tile([P, BANK], F32, tag="bank", name="col_sums")
+            for c in range(16):
                 if s < Z_ITEMS:
-                    nc.tensor.matmul(
-                        out=col_sums[s][:, 0:SUM_COLS], lhsT=raw[s][:, c * P : (c + 1) * P], rhs=pick_z[:], start=(c == 0), stop=False
-                    )
+                    pick = pick_z[:]
                 else:
-                    g = c // 2
+                    pick = pick_g[:, c // 2 * SUM_COLS : (c // 2 + 1) * SUM_COLS]
+                nc.tensor.matmul(
+                    out=col_sums[s][:, 0:SUM_COLS],
+                    lhsT=weights[s][:, c * P : (c + 1) * P],
+                    rhs=pick,
+                    start=(c == 0),
+                    stop=(c == 15 and s >= Z_ITEMS),
+                )
+            for c in range(16):
+                if s < Z_ITEMS:
                     nc.tensor.matmul(
                         out=col_sums[s][:, 0:SUM_COLS],
-                        lhsT=raw[s][:, c * P : (c + 1) * P],
-                        rhs=pick_g[:, g * SUM_COLS : (g + 1) * SUM_COLS],
-                        start=(c == 0),
+                        lhsT=low[s][:, c * P : (c + 1) * P],
+                        rhs=pick_z2[:],
+                        start=False,
                         stop=(c == 15),
                     )
-
-        def sums_low(s, h):
-            for c in range(8 * h, 8 * h + 8):
-                if s < Z_ITEMS:
-                    nc.tensor.matmul(
-                        out=col_sums[s][:, 0:SUM_COLS], lhsT=low[s][:, c * P : (c + 1) * P], rhs=pick_z2[:], start=False, stop=(c == 15)
-                    )
                 else:
-                    gh = c % 2
                     nc.tensor.matmul(
                         out=col_sums[s][:, 8 : 8 + SUM_COLS],
                         lhsT=low[s][:, c * P : (c + 1) * P],
-                        rhs=pick_g[:, gh * SUM_COLS : (gh + 1) * SUM_COLS],
+                        rhs=pick_g[:, c % 2 * SUM_COLS : (c % 2 + 1) * SUM_COLS],
                         start=(c == 0),
                         stop=(c == 15),
                     )
 
-        def sums_out(s):
+        def column_sums_out(s):
             width = 8 if s < Z_ITEMS else 10
             nc.scalar.copy(out=col_sums_sb[s % 2][:, 0:width], in_=col_sums[s][:, 0:width])
 
         def sum_blocks(s):
-            block_sums[s] = psum.tile([P, 512], F32, tag="bank", name="block_sums")
+            block_sums[s] = psum.tile([P, BANK], F32, tag="bank", name="block_sums")
             nc.tensor.matmul(
-                out=block_sums[s][:, 0:64], lhsT=ones_f[:], rhs=col_sums_sb[s % 2][:], start=True, stop=True
+                out=block_sums[s][:, 0:TOTAL_COLS], lhsT=ones_f[:], rhs=col_sums_sb[s % 2][:], start=True, stop=True
             )
             if s >= Z_ITEMS:
                 nc.tensor.matmul(
-                    out=block_sums[s][:, 8:64], lhsT=same_g4[:], rhs=col_sums_sb[s % 2][:, 8:64], start=True, stop=True
+                    out=block_sums[s][:, 8:TOTAL_COLS],
+                    lhsT=same_g4[:],
+                    rhs=col_sums_sb[s % 2][:, 8:TOTAL_COLS],
+                    start=True,
+                    stop=True,
                 )
 
-        def gain_of(s):
+        def own_factor(s):
             width = 8 if s < Z_ITEMS else 10
             spare = work.tile([P, 10], F32, tag="spare", name="spare")
             nc.vector.scalar_tensor_tensor(
@@ -187,21 +192,22 @@ def tile_bqqlinear_pa_kernel(tc, x_q, Y_fp, Z_fp, a_core, out):
                 in1=own[:, 0:width],
                 op0=ALU.mult,
                 op1=ALU.mult,
-                accum_out=gain[:, s : s + 1],
+                accum_out=factor[:, s : s + 1],
             )
 
-        def scale(s):
+        def apply_factor(s):
             part = low[s][:] if s < Z_ITEMS else w_grouped[:, (s - Z_ITEMS) * 2048 : (s - Z_ITEMS + 1) * 2048]
             nc.vector.tensor_scalar(
-                out=part, in0=part, scalar1=-TINY, scalar2=gain[:, s : s + 1], op0=ALU.max, op1=ALU.mult
+                out=part, in0=part, scalar1=-TINY, scalar2=factor[:, s : s + 1], op0=ALU.max, op1=ALU.mult
             )
 
-        def transpose_item(s, h):
+        def transpose_item(s):
             words = low[s][:].bitcast(F32)
-            banks[s, h] = psum.tile([P, 512], F32, tag="bank", name="bank_w")
-            for i in range(4):
-                first = (h * 4 + i) * P
-                nc.tensor.transpose(banks[s, h][:, i * P : (i + 1) * P], words[:, first : first + P], ident_f[:])
+            for h in range(2):
+                banks[s, h] = psum.tile([P, BANK], F32, tag="bank", name="bank_w")
+                for i in range(4):
+                    first = (h * 4 + i) * P
+                    nc.tensor.transpose(banks[s, h][:, i * P : (i + 1) * P], words[:, first : first + P], ident_f[:])
 
         def item_out(s):
             for h in range(2):
@@ -214,9 +220,9 @@ def tile_bqqlinear_pa_kernel(tc, x_q, Y_fp, Z_fp, a_core, out):
                         in_=bank[:].rearrange("q (y pj k lg) -> q k pj lg y", y=4, pj=2, k=NK),
                     )
                 else:
-                    first = ((s - Z_ITEMS) * 2 + h) * 512
+                    first = ((s - Z_ITEMS) * 2 + h) * BANK
                     nc.scalar.copy(
-                        out=w_grouped[:].bitcast(F32)[:, first : first + 512].rearrange("q (x r w) -> q x r w", x=2, w=2),
+                        out=w_grouped[:].bitcast(F32)[:, first : first + BANK].rearrange("q (x r w) -> q x r w", x=2, w=2),
                         in_=bank[:].rearrange("q (x w r) -> q x r w", x=2, w=2),
                     )
 
@@ -241,20 +247,25 @@ def tile_bqqlinear_pa_kernel(tc, x_q, Y_fp, Z_fp, a_core, out):
         t_rows = {}
         o_sb = {}
         grouped = {}
+        t_ps = {}
+        o_ps = {}
 
-        def transpose_rows(key, rows, h):
-            banks[key, h] = psum.tile([P, 512], F32, tag="bank", name="bank_t")
-            for s in range(4):
-                first = h * 512 + s * P
-                nc.tensor.transpose(banks[key, h][:, s * P : (s + 1) * P], rows[:, first : first + P], ident_f[:])
+        def transpose_rows(key, rows):
+            for h in range(2):
+                banks[key, h] = psum.tile([P, BANK], F32, tag="bank", name="bank_t")
+                for i in range(4):
+                    first = (h * 4 + i) * P
+                    nc.tensor.transpose(banks[key, h][:, i * P : (i + 1) * P], rows[:, first : first + P], ident_f[:])
 
-        def rows_out(key, h, copy):
-            if h == 0:
-                grouped[key] = work.tile([P, 2048], BF16, align_bytes=64, tag="grouped", name="grouped", bufs=5)
-            copy(
-                out=grouped[key][:].bitcast(F32)[:, h * 512 : (h + 1) * 512].rearrange("q (c b w) -> q c b w", c=2, w=2),
-                in_=banks[key, h][:].rearrange("q (c w b) -> q c b w", c=2, w=2),
-            )
+        def rows_out(key, copy):
+            grouped[key] = work.tile([P, 2048], BF16, align_bytes=64, tag="grouped", name="grouped", bufs=5)
+            for h in range(2):
+                copy(
+                    out=grouped[key][:]
+                    .bitcast(F32)[:, h * BANK : (h + 1) * BANK]
+                    .rearrange("q (c b w) -> q c b w", c=2, w=2),
+                    in_=banks[key, h][:].rearrange("q (c w b) -> q c b w", c=2, w=2),
+                )
 
         def quantise_rows(key, h):
             kind, n = key
@@ -267,11 +278,8 @@ def tile_bqqlinear_pa_kernel(tc, x_q, Y_fp, Z_fp, a_core, out):
                 in_=grouped[key][:, h * 1024 : (h + 1) * 1024],
             )
 
-        t_ps = {}
-        o_ps = {}
-
         def first_matmul(n, k):
-            t_ps[n, k] = psum.tile([P, 512], F32, tag="bank", name="t_ps")
+            t_ps[n, k] = psum.tile([P, BANK], F32, tag="bank", name="t_ps")
             nc.tensor.matmul_mx(
                 out=t_ps[n, k][:],
                 lhsT=codes["x", n][:, k * P : (k + 1) * P].bitcast(FP8X4),
@@ -282,16 +290,16 @@ def tile_bqqlinear_pa_kernel(tc, x_q, Y_fp, Z_fp, a_core, out):
                 stop=True,
             )
 
-        def t_out(n, k, copy):
+        def t_out(n, k):
             if k == 0:
                 t_rows[n] = work.tile([P, 2048], BF16, tag="t_rows", name="t_rows", bufs=3)
-            copy(
+            nc.scalar.copy(
                 out=t_rows[n][:].rearrange("b (jw p k y) -> b jw p k y", jw=8, p=NP, k=NK)[:, :, :, k, :],
                 in_=t_ps[n, k][:].rearrange("b (p jw y) -> b jw p y", p=NP, jw=8),
             )
 
         def second_matmul(n, j):
-            o_ps[n, j] = psum.tile([P, 512], F32, tag="bank", name="o_ps")
+            o_ps[n, j] = psum.tile([P, BANK], F32, tag="bank", name="o_ps")
             nc.tensor.matmul_mx(
                 out=o_ps[n, j][:],
                 lhsT=codes["t", n][:, j * P : (j + 1) * P].bitcast(FP8X4),
@@ -302,17 +310,16 @@ def tile_bqqlinear_pa_kernel(tc, x_q, Y_fp, Z_fp, a_core, out):
                 stop=True,
             )
 
-        def o_out(n, j, copy):
+        def o_out(n, j):
             if j == 0:
                 o_sb[n] = work.tile([P, NJ * M], F32, tag="o_sb", name="o_sb", bufs=3)
+            on_vector = (j % 2 == 1 or (j == 2 and n % 3 == 0)) and n != B_TILES - 2
+            copy = nc.vector.tensor_copy if on_vector else nc.scalar.copy
             copy(
                 out=o_sb[n][:, j * M : (j + 1) * M].rearrange("b (r mc) -> b r mc", mc=4),
                 in_=o_ps[n, j][:].rearrange("b (mc r) -> b r mc", mc=4),
             )
             nc.sync.dma_start(out=out_rows[n * P : (n + 1) * P, j * M : (j + 1) * M], in_=o_sb[n][:, j * M : (j + 1) * M])
-
-        def is_item(s):
-            return 0 <= s < ITEMS
 
         def is_z(s):
             return 0 <= s < Z_ITEMS
@@ -320,96 +327,71 @@ def tile_bqqlinear_pa_kernel(tc, x_q, Y_fp, Z_fp, a_core, out):
         def is_y(s):
             return Z_ITEMS <= s < ITEMS
 
+        def is_item(s):
+            return 0 <= s < ITEMS
+
         def is_tile(n):
             return 0 <= n < B_TILES
 
-        scalar, vector = nc.scalar.copy, nc.vector.tensor_copy
-        for step in range(ITEMS + 3):
+        for step in range(ITEMS + 2):
             if step == 3:
                 own_a()
-            if is_item(step):
-                clamp_above(step)
+            if step == 0:
+                clamp_above(0)
             if is_y(step - 2):
-                scale(step - 2)
+                apply_factor(step - 2)
             if is_item(step - 1):
                 sum_blocks(step - 1)
             if is_item(step):
-                sums_raw(step, 0)
-            if is_item(step):
-                sums_raw(step, 1)
-            if is_item(step):
-                sums_low(step, 0)
-            if is_item(step):
-                sums_low(step, 1)
+                column_sums(step)
             if is_item(step - 1):
-                gain_of(step - 1)
+                own_factor(step - 1)
             if is_tile(step - 1):
-                transpose_rows(("x", step - 1), x_sb[step - 1][:].bitcast(F32), 0)
-            if is_tile(step - 1):
-                transpose_rows(("x", step - 1), x_sb[step - 1][:].bitcast(F32), 1)
+                transpose_rows(("x", step - 1), x_sb[step - 1][:].bitcast(F32))
             if is_tile(step - 2):
                 quantise_rows(("x", step - 2), 0)
             if is_z(step - 1):
-                scale(step - 1)
+                apply_factor(step - 1)
             if is_z(step - 3):
                 quantise_item(step - 3)
+            if is_item(step + 1):
+                clamp_above(step + 1)
             if is_tile(step - 2):
                 quantise_rows(("x", step - 2), 1)
             if is_y(step - 2):
                 quantise_item(step - 2)
             if is_item(step):
-                sums_out(step)
+                column_sums_out(step)
             if is_y(step):
-                transpose_item(step, 0)
-            if is_y(step):
-                transpose_item(step, 1)
+                transpose_item(step)
             if is_z(step - 1):
-                transpose_item(step - 1, 0)
-            if is_z(step - 1):
-                transpose_item(step - 1, 1)
+                transpose_item(step - 1)
             if is_tile(step - 1):
-                rows_out(("x", step - 1), 0, vector if step >= 8 else scalar)
-            if is_tile(step - 1):
-                rows_out(("x", step - 1), 1, vector if step >= 8 else scalar)
+                rows_out(("x", step - 1), nc.vector.tensor_copy if step - 1 == B_TILES - 1 else nc.scalar.copy)
             if is_y(step):
                 item_out(step)
             if is_z(step - 1):
                 item_out(step - 1)
 
-        for n in range(B_TILES + 3):
-            if is_tile(n):
+        for step in range(B_TILES + 3):
+            if is_tile(step):
                 for k in (0, 1):
-                    first_matmul(n, k)
-            if is_tile(n - 3):
-                for j in (0, 1):
-                    second_matmul(n - 3, j)
-            if is_tile(n - 3):
-                for j in (2, 3):
-                    second_matmul(n - 3, j)
-            if is_tile(n - 3):
-                for j in (0, 1):
-                    o_out(n - 3, j, vector if (j % 2 or (j == 2 and (n - 3) % 3 == 0)) and n - 3 != B_TILES - 2 else scalar)
-            if is_tile(n - 2):
-                quantise_rows(("t", n - 2), 0)
-            if is_tile(n - 3):
-                for j in (2, 3):
-                    o_out(n - 3, j, vector if (j % 2 or (j == 2 and (n - 3) % 3 == 0)) and n - 3 != B_TILES - 2 else scalar)
-            if is_tile(n - 2):
-                quantise_rows(("t", n - 2), 1)
-            if is_tile(n):
+                    first_matmul(step, k)
+            if is_tile(step - 3):
+                for j in range(NJ):
+                    second_matmul(step - 3, j)
+            for h in range(2):
+                if is_tile(step - 3):
+                    for j in (2 * h, 2 * h + 1):
+                        o_out(step - 3, j)
+                if is_tile(step - 2):
+                    quantise_rows(("t", step - 2), h)
+            if is_tile(step):
                 for k in (2, 3):
-                    first_matmul(n, k)
-            if is_tile(n - 1):
-                transpose_rows(("t", n - 1), t_rows[n - 1][:].bitcast(F32), 0)
-            if is_tile(n - 1):
-                transpose_rows(("t", n - 1), t_rows[n - 1][:].bitcast(F32), 1)
-            if is_tile(n - 1):
-                rows_out(("t", n - 1), 0, vector)
-            if is_tile(n - 1):
-                rows_out(("t", n - 1), 1, vector)
-            if is_tile(n):
-                for k in (0, 1):
-                    t_out(n, k, scalar)
-            if is_tile(n):
-                for k in (2, 3):
-                    t_out(n, k, scalar)
+                    first_matmul(step, k)
+            if is_tile(step - 1):
+                transpose_rows(("t", step - 1), t_rows[step - 1][:].bitcast(F32))
+                rows_out(("t", step - 1), nc.vector.tensor_copy)
+            if is_tile(step):
+                for k in range(NK):
+                    t_out(step, k)

from contextlib import ExitStack

import concourse.mybir as mybir
from concourse.masks import make_identity

BF16 = mybir.dt.bfloat16
F32 = mybir.dt.float32
U32 = mybir.dt.uint32
U8 = mybir.dt.uint8
FP8X4 = mybir.dt.float8_e4m3fn_x4
ALU = mybir.AluOpType
AX = mybir.AxisListType

P = 128
NP, NJ, NK = 2, 4, 4
PAIRS = NP * NK
M, L, N = 512, 64, 512
B = 1024
B_TILES = B // P
BANK = 512
BLOCK_ELEMS = M * L
TINY = 2.0**-100
Z_ITEMS = 4
ITEMS = Z_ITEMS + NJ
SUM_COLS = 48
TOTAL_COLS = 64
FLOPS = 2 * (2 * B * N * NP * NJ * NK * L)


def tile_bqqlinear_pa_kernel(tc, x_q, Y_fp, Z_fp, a_core, out):
    nc = tc.nc
    x_rows = x_q.flatten_outer_dims()
    out_rows = out.rearrange("b j m -> b (j m)")
    z_chunks = Z_fp.rearrange("p j k l n -> (p j k l) n").rearrange("(s r x) n -> s r (x n)", s=Z_ITEMS, r=P)

    with ExitStack() as ctx:
        const = ctx.enter_context(tc.tile_pool(name="const", bufs=1))
        work = ctx.enter_context(tc.tile_pool(name="work", bufs=2))
        psum = ctx.enter_context(tc.psum_pool(name="psum", bufs=8))
        ctx.enter_context(tc.manual_schedule())

        a_all = const.tile([P, NP * NJ * NK], BF16)
        weights = [const.tile([P, 2048], BF16, name="weights%d" % s) for s in range(ITEMS)]
        x_sb = [const.tile([P, NK * N], BF16, name="x_sb%d" % n) for n in range(B_TILES)]

        def load_item(s):
            if s < Z_ITEMS:
                nc.sync.dma_start(out=weights[s][:], in_=z_chunks[s])
            else:
                with nc.allow_non_contiguous_dma(reason="rows of four m, 256 bfloat16 values"):
                    for p in range(NP):
                        nc.sync.dma_start(
                            out=weights[s][:, p * 1024 : (p + 1) * 1024].rearrange("r (k x) -> r k x", k=NK),
                            in_=Y_fp[p, s - Z_ITEMS].rearrange("k (r mc) l -> r k (mc l)", mc=4),
                        )

        load_item(0)
        for i in range(ITEMS):
            if i + 1 < ITEMS:
                load_item(i + 1)
            nc.sync.dma_start(out=x_sb[i][:], in_=x_rows[i * P : (i + 1) * P, :])
            if i == 1:
                nc.sync.dma_start(out=a_all[:], in_=a_core.rearrange("p j k -> (p j k)").partition_broadcast(P))

        ident_f = const.tile([P, P], F32)
        make_identity(nc, ident_f[:])
        ones_f = const.tile([P, P], F32)
        nc.vector.memset(ones_f[:], 1.0)
        pick_g = const.tile([P, PAIRS * SUM_COLS], BF16)
        nc.vector.memset(pick_g[:], 0.0)
        nc.vector.memset(pick_g[:, 0 : PAIRS * SUM_COLS : SUM_COLS + 1], 1.0)
        same_g4 = const.tile([P, P], F32)
        nc.vector.memset(same_g4[:], 0.0)
        for i in range(4):
            nc.vector.memset(
                same_g4[32 * i : 32 * i + 32, :].rearrange("x (h g lam) -> x h g lam", h=2, g=4)[:, :, i, :], 1.0
            )
        own = const.tile([P, 10], F32)
        nc.vector.tensor_reduce(
            out=own[:, 0:8], in_=ident_f[:].rearrange("q (g lam) -> q g lam", g=PAIRS), axis=AX.X, op=ALU.add
        )
        halves = const.tile([P, 2], F32)
        nc.vector.tensor_reduce(
            out=halves[:], in_=ident_f[:].rearrange("q (h x) -> q h x", h=2), axis=AX.X, op=ALU.add
        )
        pick_z = const.tile([P, SUM_COLS], BF16)
        nc.vector.memset(pick_z[:], 0.0)
        nc.vector.tensor_copy(out=pick_z[:, 0:8], in_=own[:, 0:8])
        pick_z2 = const.tile([P, SUM_COLS], BF16)
        nc.vector.memset(pick_z2[:], 0.0)
        nc.vector.tensor_scalar(out=pick_z2[:, 0:8], in0=own[:, 0:8], scalar1=-2.0, scalar2=None, op0=ALU.mult)
        nc.vector.tensor_scalar(out=own[:, 8:10], in0=halves[:], scalar1=-2.0, scalar2=None, op0=ALU.mult)
        a_pick = const.tile([P, NJ * PAIRS], F32)
        a_sum = const.tile([P, NJ], F32)
        a_own = const.tile([P, NJ], F32)

        def own_a():
            nc.vector.tensor_tensor(
                out=a_pick[:].rearrange("q (j p k) -> q j p k", j=NJ, p=NP),
                in0=a_all[:].rearrange("q (p j k) -> q j p k", p=NP, j=NJ),
                in1=own[:, 0:8].rearrange("q (p k) -> q p k", p=NP).unsqueeze(1).to_broadcast([P, NJ, NP, NK]),
                op=ALU.mult,
            )
            nc.vector.tensor_reduce(
                out=a_sum[:], in_=a_pick[:].rearrange("q (j g) -> q j g", j=NJ), axis=AX.X, op=ALU.add
            )
            nc.vector.tensor_scalar(
                out=a_own[:], in0=a_sum[:], scalar1=1.0 / (TINY * BLOCK_ELEMS), scalar2=None, op0=ALU.mult
            )

        z_grouped = [const.tile([P, 2048], BF16, align_bytes=64, name="z_grouped%d" % s) for s in range(Z_ITEMS)]
        z_codes = const.tile([P, NK * 512], U32, align_bytes=256)
        z_scales = const.tile([P, NK * 512], U8, align_bytes=256)
        w_grouped = const.tile([P, NJ * 2048], BF16, align_bytes=64)
        w_codes = const.tile([P, NJ * 512], U32, align_bytes=256)
        w_scales = const.tile([P, NJ * 512], U8, align_bytes=256)
        factor = const.tile([P, ITEMS], F32)
        low = {}
        col_sums = {}
        col_sums_sb = [const.tile([P, TOTAL_COLS], F32, name="col_sums_sb%d" % i) for i in range(2)]
        for i in range(2):
            nc.vector.memset(col_sums_sb[i][:], 0.0)
        block_sums = {}
        banks = {}

        def clamp_above(s):
            low[s] = work.tile([P, 2048], BF16, tag="low", name="low", bufs=5)
            if s < Z_ITEMS:
                clamped, values = low[s][:], weights[s][:]
            else:
                clamped = low[s][:].rearrange("r (mw g y) -> r mw g y", mw=8, g=PAIRS)
                values = weights[s][:].rearrange("r (g mw y) -> r mw g y", mw=8, g=PAIRS)
            nc.vector.tensor_scalar(out=clamped, in0=values, scalar1=TINY, scalar2=None, op0=ALU.min)

        def column_sums(s):
            col_sums[s] = psum.tile([P, BANK], F32, tag="bank", name="col_sums")
            for c in range(16):
                if s < Z_ITEMS:
                    pick = pick_z[:]
                else:
                    pick = pick_g[:, c // 2 * SUM_COLS : (c // 2 + 1) * SUM_COLS]
                nc.tensor.matmul(
                    out=col_sums[s][:, 0:SUM_COLS],
                    lhsT=weights[s][:, c * P : (c + 1) * P],
                    rhs=pick,
                    start=(c == 0),
                    stop=(c == 15 and s >= Z_ITEMS),
                )
            for c in range(16):
                if s < Z_ITEMS:
                    nc.tensor.matmul(
                        out=col_sums[s][:, 0:SUM_COLS],
                        lhsT=low[s][:, c * P : (c + 1) * P],
                        rhs=pick_z2[:],
                        start=False,
                        stop=(c == 15),
                    )
                else:
                    nc.tensor.matmul(
                        out=col_sums[s][:, 8 : 8 + SUM_COLS],
                        lhsT=low[s][:, c * P : (c + 1) * P],
                        rhs=pick_g[:, c % 2 * SUM_COLS : (c % 2 + 1) * SUM_COLS],
                        start=(c == 0),
                        stop=(c == 15),
                    )

        def column_sums_out(s):
            width = 8 if s < Z_ITEMS else 10
            nc.scalar.copy(out=col_sums_sb[s % 2][:, 0:width], in_=col_sums[s][:, 0:width])

        def sum_blocks(s):
            block_sums[s] = psum.tile([P, BANK], F32, tag="bank", name="block_sums")
            nc.tensor.matmul(
                out=block_sums[s][:, 0:TOTAL_COLS], lhsT=ones_f[:], rhs=col_sums_sb[s % 2][:], start=True, stop=True
            )
            if s >= Z_ITEMS:
                nc.tensor.matmul(
                    out=block_sums[s][:, 8:TOTAL_COLS],
                    lhsT=same_g4[:],
                    rhs=col_sums_sb[s % 2][:, 8:TOTAL_COLS],
                    start=True,
                    stop=True,
                )

        def own_factor(s):
            width = 8 if s < Z_ITEMS else 10
            spare = work.tile([P, 10], F32, tag="spare", name="spare")
            nc.vector.scalar_tensor_tensor(
                out=spare[:, 0:width],
                in0=block_sums[s][:, 0:width],
                scalar=1.0 / (TINY * BLOCK_ELEMS) if s < Z_ITEMS else a_own[:, s - Z_ITEMS : s - Z_ITEMS + 1],
                in1=own[:, 0:width],
                op0=ALU.mult,
                op1=ALU.mult,
                accum_out=factor[:, s : s + 1],
            )

        def apply_factor(s):
            part = low[s][:] if s < Z_ITEMS else w_grouped[:, (s - Z_ITEMS) * 2048 : (s - Z_ITEMS + 1) * 2048]
            nc.vector.tensor_scalar(
                out=part, in0=part, scalar1=-TINY, scalar2=factor[:, s : s + 1], op0=ALU.max, op1=ALU.mult
            )

        def transpose_item(s):
            words = low[s][:].bitcast(F32)
            for h in range(2):
                banks[s, h] = psum.tile([P, BANK], F32, tag="bank", name="bank_w")
                for i in range(4):
                    first = (h * 4 + i) * P
                    nc.tensor.transpose(banks[s, h][:, i * P : (i + 1) * P], words[:, first : first + P], ident_f[:])

        def item_out(s):
            for h in range(2):
                bank = banks[s, h]
                if s < Z_ITEMS:
                    nc.scalar.copy(
                        out=z_grouped[s][:]
                        .bitcast(F32)
                        .rearrange("q (k pj lg h y) -> q k pj lg h y", k=NK, pj=2, h=2, y=4)[:, :, :, :, h, :],
                        in_=bank[:].rearrange("q (y pj k lg) -> q k pj lg y", y=4, pj=2, k=NK),
                    )
                else:
                    first = ((s - Z_ITEMS) * 2 + h) * BANK
                    nc.scalar.copy(
                        out=w_grouped[:].bitcast(F32)[:, first : first + BANK].rearrange("q (x r w) -> q x r w", x=2, w=2),
                        in_=bank[:].rearrange("q (x w r) -> q x r w", x=2, w=2),
                    )

        def quantise_item(s):
            if s < Z_ITEMS:
                for k in range(NK):
                    nc.vector.quantize_mx(
                        out=z_codes[:, k * 512 + s * P : k * 512 + (s + 1) * P].bitcast(FP8X4),
                        scales=z_scales[:, k * 512 + s * P : k * 512 + (s + 1) * P],
                        in_=z_grouped[s][:, k * 512 : (k + 1) * 512],
                    )
            else:
                j = s - Z_ITEMS
                nc.vector.quantize_mx(
                    out=w_codes[:, j * 512 : (j + 1) * 512].bitcast(FP8X4),
                    scales=w_scales[:, j * 512 : (j + 1) * 512],
                    in_=w_grouped[:, j * 2048 : (j + 1) * 2048],
                )

        codes = {}
        scales = {}
        t_rows = {}
        o_sb = {}
        grouped = {}
        t_ps = {}
        o_ps = {}

        def transpose_rows(key, rows):
            for h in range(2):
                banks[key, h] = psum.tile([P, BANK], F32, tag="bank", name="bank_t")
                for i in range(4):
                    first = (h * 4 + i) * P
                    nc.tensor.transpose(banks[key, h][:, i * P : (i + 1) * P], rows[:, first : first + P], ident_f[:])

        def rows_out(key, copy):
            grouped[key] = work.tile([P, 2048], BF16, align_bytes=64, tag="grouped", name="grouped", bufs=5)
            for h in range(2):
                copy(
                    out=grouped[key][:]
                    .bitcast(F32)[:, h * BANK : (h + 1) * BANK]
                    .rearrange("q (c b w) -> q c b w", c=2, w=2),
                    in_=banks[key, h][:].rearrange("q (c w b) -> q c b w", c=2, w=2),
                )

        def quantise_rows(key, h):
            kind, n = key
            if h == 0:
                codes[key] = work.tile([P, 512], U32, align_bytes=256, tag="codes_" + kind, name="codes", bufs=8)
                scales[key] = work.tile([P, 512], U8, align_bytes=256, tag="scales_" + kind, name="scales", bufs=8)
            nc.vector.quantize_mx(
                out=codes[key][:, h * 256 : (h + 1) * 256].bitcast(FP8X4),
                scales=scales[key][:, h * 256 : (h + 1) * 256],
                in_=grouped[key][:, h * 1024 : (h + 1) * 1024],
            )

        def first_matmul(n, k):
            t_ps[n, k] = psum.tile([P, BANK], F32, tag="bank", name="t_ps")
            nc.tensor.matmul_mx(
                out=t_ps[n, k][:],
                lhsT=codes["x", n][:, k * P : (k + 1) * P].bitcast(FP8X4),
                lhsT_scale=scales["x", n][:, k * P : (k + 1) * P],
                rhs=z_codes[:, k * 512 : (k + 1) * 512].bitcast(FP8X4),
                rhs_scale=z_scales[:, k * 512 : (k + 1) * 512],
                start=True,
                stop=True,
            )

        def t_out(n, k):
            if k == 0:
                t_rows[n] = work.tile([P, 2048], BF16, tag="t_rows", name="t_rows", bufs=3)
            nc.scalar.copy(
                out=t_rows[n][:].rearrange("b (jw p k y) -> b jw p k y", jw=8, p=NP, k=NK)[:, :, :, k, :],
                in_=t_ps[n, k][:].rearrange("b (p jw y) -> b jw p y", p=NP, jw=8),
            )

        def second_matmul(n, j):
            o_ps[n, j] = psum.tile([P, BANK], F32, tag="bank", name="o_ps")
            nc.tensor.matmul_mx(
                out=o_ps[n, j][:],
                lhsT=codes["t", n][:, j * P : (j + 1) * P].bitcast(FP8X4),
                lhsT_scale=scales["t", n][:, j * P : (j + 1) * P],
                rhs=w_codes[:, j * 512 : (j + 1) * 512].bitcast(FP8X4),
                rhs_scale=w_scales[:, j * 512 : (j + 1) * 512],
                start=True,
                stop=True,
            )

        def o_out(n, j):
            if j == 0:
                o_sb[n] = work.tile([P, NJ * M], F32, tag="o_sb", name="o_sb", bufs=3)
            on_vector = (j % 2 == 1 or (j == 2 and n % 3 == 0)) and n != B_TILES - 2
            copy = nc.vector.tensor_copy if on_vector else nc.scalar.copy
            copy(
                out=o_sb[n][:, j * M : (j + 1) * M].rearrange("b (r mc) -> b r mc", mc=4),
                in_=o_ps[n, j][:].rearrange("b (mc r) -> b r mc", mc=4),
            )
            nc.sync.dma_start(out=out_rows[n * P : (n + 1) * P, j * M : (j + 1) * M], in_=o_sb[n][:, j * M : (j + 1) * M])

        def is_z(s):
            return 0 <= s < Z_ITEMS

        def is_y(s):
            return Z_ITEMS <= s < ITEMS

        def is_item(s):
            return 0 <= s < ITEMS

        def is_tile(n):
            return 0 <= n < B_TILES

        for step in range(ITEMS + 2):
            if step == 3:
                own_a()
            if step == 0:
                clamp_above(0)
            if is_y(step - 2):
                apply_factor(step - 2)
            if is_item(step - 1):
                sum_blocks(step - 1)
            if is_item(step):
                column_sums(step)
            if is_item(step - 1):
                own_factor(step - 1)
            if is_tile(step - 1):
                transpose_rows(("x", step - 1), x_sb[step - 1][:].bitcast(F32))
            if is_tile(step - 2):
                quantise_rows(("x", step - 2), 0)
            if is_z(step - 1):
                apply_factor(step - 1)
            if is_z(step - 3):
                quantise_item(step - 3)
            if is_item(step + 1):
                clamp_above(step + 1)
            if is_tile(step - 2):
                quantise_rows(("x", step - 2), 1)
            if is_y(step - 2):
                quantise_item(step - 2)
            if is_item(step):
                column_sums_out(step)
            if is_y(step):
                transpose_item(step)
            if is_z(step - 1):
                transpose_item(step - 1)
            if is_tile(step - 1):
                rows_out(("x", step - 1), nc.vector.tensor_copy if step - 1 == B_TILES - 1 else nc.scalar.copy)
            if is_y(step):
                item_out(step)
            if is_z(step - 1):
                item_out(step - 1)

        for step in range(B_TILES + 3):
            if is_tile(step):
                for k in (0, 1):
                    first_matmul(step, k)
            if is_tile(step - 3):
                for j in range(NJ):
                    second_matmul(step - 3, j)
            for h in range(2):
                if is_tile(step - 3):
                    for j in (2 * h, 2 * h + 1):
                        o_out(step - 3, j)
                if is_tile(step - 2):
                    quantise_rows(("t", step - 2), h)
            if is_tile(step):
                for k in (2, 3):
                    first_matmul(step, k)
            if is_tile(step - 1):
                transpose_rows(("t", step - 1), t_rows[step - 1][:].bitcast(F32))
                rows_out(("t", step - 1), nc.vector.tensor_copy)
            if is_tile(step):
                for k in range(NK):
                    t_out(step, k)
